import numpy as np
import ml_dtypes


def mxq(x, axis, fmt="e4m3"):
    dtype, down = {"e4m3": (ml_dtypes.float8_e4m3fn, 7), "e5m2": (ml_dtypes.float8_e5m2, 14)}[fmt]
    v = np.moveaxis(np.asarray(x, np.float32).astype(ml_dtypes.bfloat16).astype(np.float64), axis, -1)
    blocks = v.reshape(v.shape[:-1] + (-1, 32))
    amax = np.abs(blocks).max(-1, keepdims=True)
    byte = np.maximum(np.where(amax > 0, np.frexp(amax)[1] - 1 + 127, 0) - down, 1)
    scale = np.exp2(byte - 127.0)
    codes = (blocks / scale).astype(np.float32).astype(dtype).astype(np.float64)
    return np.moveaxis((codes * scale).reshape(v.shape), -1, axis)


WIDE = False


def mx_kscale(k):
    if not WIDE:
        return np.ones(k)
    levels = np.array([10, -10, 5, -5, 0])
    a = np.random.permutation(np.resize(levels, k // 512 * 4)).reshape(k // 512, 4)
    idx = np.arange(k)
    return np.exp2(a[idx // 512, idx % 128 // 32])


BF16 = ml_dtypes.bfloat16


def bf(x):
    return np.asarray(x, np.float32).astype(BF16)


def f64(x):
    return np.asarray(x).astype(np.float64)


E2M1 = np.array([0.0, 0.5, 1.0, 1.5, 2.0, 3.0, 4.0, 6.0, -0.0, -0.5, -1.0, -1.5, -2.0, -3.0, -4.0, -6.0])


def pack_weight(w, fmt):
    k, n = w.shape
    w = f64(bf(w)).reshape(k // 32, 32, n)
    amax = np.abs(w).max(1)
    if fmt == "e4m3":
        byte = np.frexp(amax)[1] - 1 + 127 - 7
    else:
        mant, ex = np.frexp(amax / 6.0)
        byte = np.where(mant > 0.5, ex, ex - 1) + 127
    byte = np.clip(np.where(amax > 0, byte, 1), 1, 254)
    scaled = (w * np.exp2(127.0 - byte)[:, None, :]).reshape(k, n).astype(np.float32)
    by_word = np.ascontiguousarray(scaled.reshape(k // 512, 128, 4, n).transpose(0, 1, 3, 2))
    if fmt == "e4m3":
        words = by_word.astype(ml_dtypes.float8_e4m3fn).view(np.uint8)
    else:
        c = by_word.astype(ml_dtypes.float4_e2m1fn).view(np.uint8) & 0xF
        words = c[..., 0::2] | (c[..., 1::2] << 4)
    return np.ascontiguousarray(words), np.ascontiguousarray(byte.astype(np.uint8).reshape(k // 512, 16, n))


def unpack_weight(words, scales, fmt):
    g, p, n, _ = words.shape
    if fmt == "e4m3":
        vals = np.ascontiguousarray(words).view(ml_dtypes.float8_e4m3fn).astype(np.float64)
    else:
        nib = np.empty((g, p, n, 4), np.uint8)
        nib[..., 0::2] = words & 0xF
        nib[..., 1::2] = words >> 4
        vals = E2M1[nib]
    vals = vals * np.repeat(np.exp2(scales.astype(np.float64) - 127.0), 8, axis=1)[..., None]
    return vals.transpose(0, 1, 3, 2).reshape(g * 512, n)


B, D, N, G, K = 256, 128, 2048, 60, 4
BLK = 32
F = G + K
T0, T1 = -1.0, (G - BLK) / BLK


def silu(v):
    return v / (1.0 + np.exp(-v))


def bspline_basis(x, t, k):
    xb = x[..., None]
    b = np.where((xb >= t[:-1]) & (xb < t[1:]), 1.0, 0.0)
    T = t.shape[0]
    for p in range(2, k + 1):
        n = T - p
        d1 = t[p - 1:p - 1 + n] - t[:n]
        d2 = t[p:p + n] - t[1:1 + n]
        w1 = np.where(d1 > 0, (xb - t[:n]) / np.where(d1 > 0, d1, 1.0), 0.0)
        w2 = np.where(d2 > 0, (t[p:p + n] - xb) / np.where(d2 > 0, d2, 1.0), 0.0)
        b = w1 * b[..., :n] + w2 * b[..., 1:n + 1]
    return b


def setup_inputs():
    x = np.random.uniform(T0, T1 - 0.01, (B, D))
    w = np.random.standard_normal((D * F, N)) * 1.4 / np.sqrt(D)
    inner = (np.arange(G + 1) - BLK) / BLK
    inner[1:-1] += np.random.uniform(-0.25, 0.25, G - 1) / BLK
    inner[BLK] = 0.0
    s = mx_kscale(D * F)
    cx = np.exp2(-np.round(0.6 * np.log2(s.max() / s.min())))
    dd = np.arange(0, D, 8)
    x[:, dd] *= cx
    w[dd * F + BLK - 1] /= cx * cx
    t = bf(np.concatenate([np.full(K - 1, T0), inner, np.full(K - 1, T1)]))
    w_words, w_scales = pack_weight(w, "e4m3")
    return {"x": bf(x), "w_words": w_words, "w_scales": w_scales, "t": t, "k": K}


def reference(x, w_words, w_scales, t, k):
    x = f64(x)
    y1 = bspline_basis(x, f64(t), k)
    y2 = np.concatenate([y1, silu(x)[..., None]], axis=2)
    y = y2.reshape(x.shape[0], -1)
    return mxq(y, 1, "e4m3") @ unpack_weight(w_words, w_scales, "e4m3")

@@ -1,0 +1,298 @@
+from contextlib import ExitStack
+
+import concourse.mybir as mybir
+from concourse.masks import make_identity
+
+F32 = mybir.dt.float32
+BF16 = mybir.dt.bfloat16
+I32 = mybir.dt.int32
+U32 = mybir.dt.uint32
+U8 = mybir.dt.uint8
+FP8X4 = mybir.dt.float8_e4m3fn_x4
+ALU = mybir.AluOpType
+ACT = mybir.ActivationFunctionType
+AX = mybir.AxisListType
+
+P = 128
+BATCH = 256
+HALVES = BATCH // P
+D = 128
+N = 2048
+PASSES = 16
+DL = 8
+JQ = 16
+PACK = 4
+N_TILE = 512
+N_TILES = N // N_TILE
+CHUNK = 4
+FLOPS = 2 * BATCH * D * 64 * N
+
+
+def tile_regular_kan_w_kernel(tc, x, w_words, w_scales, t, k, out):
+    nc = tc.nc
+    assert k == 4
+    with ExitStack() as ctx:
+        keep = ctx.enter_context(tc.tile_pool(name="keep", bufs=1))
+        work = ctx.enter_context(tc.tile_pool(name="work", bufs=2))
+        psum_acc = ctx.enter_context(tc.psum_pool(name="acc", bufs=1))
+        psum_fe = ctx.enter_context(tc.psum_pool(name="fe", bufs=4))
+
+        knots16 = keep.tile([P, 4, 16], BF16)
+        nc.vector.memset(knots16[:], 0.0)
+        nc.sync.dma_start(out=knots16[1:16, 0, 0:4], in_=t[0:60].rearrange("(q c) -> q c", c=4))
+        nc.sync.dma_start(out=knots16[0:16, 1, 0:4], in_=t[0:64].rearrange("(q c) -> q c", c=4))
+        nc.sync.dma_start(out=knots16[0:15, 2, 0:4], in_=t[4:64].rearrange("(q c) -> q c", c=4))
+        nc.sync.dma_start(out=knots16[15:16, 2, 0:3], in_=t[64:67].rearrange("(o c) -> o c", o=1))
+        x_sb = []
+        for h in range(HALVES):
+            x_half = keep.tile([P, D], BF16, name="x_half%d" % h)
+            nc.sync.dma_start(out=x_half[:], in_=x[h * P : (h + 1) * P, :])
+            x_sb.append(x_half)
+
+        w_planes = keep.tile([P, PASSES // 4, N], U8, align_bytes=64)
+        nc.vector.memset(w_planes[:].rearrange("p s n -> p (s n)").bitcast(I32), 0)
+        for slot in range(PASSES // 4):
+            for quad in range(4):
+                nc.sync.dma_start(
+                    out=w_planes[32 * quad : 32 * quad + 16, slot, :].bitcast(I32),
+                    in_=w_scales[4 * slot : 4 * slot + 4, 4 * quad : 4 * quad + 4, :].bitcast(I32),
+                )
+        w_codes = []
+        for g in range(PASSES):
+            w_pass = keep.tile([P, N], U32, name="w_pass%d" % g, align_bytes=64)
+            nc.sync.dma_start(
+                out=w_pass[:].bitcast(I32),
+                in_=w_words[g].rearrange("p n c -> p (n c)").bitcast(I32),
+            )
+            w_codes.append(w_pass)
+
+        ident = keep.tile([P, P], BF16)
+        make_identity(nc, ident[:])
+        ident_dj = ident[:].rearrange("p (a b) -> p a b", b=JQ)
+        sel = keep.tile([P, DL, JQ], BF16)
+        nc.vector.tensor_copy(out=sel[:], in_=ident[:, 0:JQ].unsqueeze(1).to_broadcast([P, DL, JQ]))
+        own_d = keep.tile([P, DL], F32)
+        nc.vector.tensor_reduce(out=own_d[:], in_=ident_dj, axis=AX.X, op=ALU.add)
+        first = keep.tile([P, 1], F32)
+        nc.vector.tensor_reduce(out=first[:], in_=ident_dj[:, :, 0], axis=AX.X, op=ALU.add)
+        later = keep.tile([P, 1], F32)
+        nc.vector.tensor_scalar(out=later[:], in0=first[:], scalar1=-1.0, scalar2=1.0, op0=ALU.mult, op1=ALU.add)
+
+        rep_ps = psum_fe.tile([P, 64], F32, tag="fe")
+        nc.tensor.matmul(
+            out=rep_ps[:],
+            lhsT=sel[:].rearrange("p a b -> p (a b)"),
+            rhs=knots16[:].rearrange("p a c -> p (a c)"),
+            start=True,
+            stop=True,
+        )
+        wn = keep.tile([P, 12], F32)
+        nc.vector.tensor_copy(
+            out=wn[:].rearrange("p (a c) -> p a c", c=4),
+            in_=rep_ps[:].rearrange("p (a c) -> p a c", c=16)[:, 0:3, 0:4],
+        )
+        prev = keep.tile([P, 9], F32)
+        nc.vector.tensor_scalar(out=prev[:], in0=wn[:, 1:10], scalar1=later[:], scalar2=None, op0=ALU.mult)
+        step = keep.tile([P, 9], F32)
+        nc.vector.tensor_tensor(out=step[:], in0=wn[:, 2:11], in1=prev[:], op=ALU.subtract)
+        step_hi = keep.tile([P, 9], BF16)
+        nc.vector.tensor_copy(out=step_hi[:], in_=step[:])
+        step_lo = keep.tile([P, 9], F32)
+        nc.vector.tensor_tensor(out=step_lo[:], in0=step[:], in1=step_hi[:], op=ALU.subtract)
+
+        sign = keep.tile([P, PACK, 6], F32)
+        nc.vector.memset(sign[:, :, 0:3], -1.0)
+        nc.vector.memset(sign[:, :, 3:6], 1.0)
+        nc.vector.tensor_scalar(out=sign[:, 0:3, :], in0=sign[:, 0:3, :], scalar1=later[:], scalar2=None, op0=ALU.mult)
+        row = keep.tile([P, PACK, 16], BF16)
+        nc.vector.memset(row[:], 0.0)
+        for tt in range(PACK):
+            nc.vector.tensor_tensor(out=row[:, tt, 0:6], in0=step_hi[:, tt : tt + 6], in1=sign[:, tt, :], op=ALU.mult)
+            nc.vector.tensor_tensor(out=row[:, tt, 6:12], in0=step_lo[:, tt : tt + 6], in1=sign[:, tt, :], op=ALU.mult)
+        nc.vector.tensor_copy(
+            out=row[:].rearrange("p a f -> p (a f)")[:, 12:64:17], in_=later[:].to_broadcast([P, PACK])
+        )
+        table = keep.tile([P, PACK, DL, 16], BF16)
+        nc.vector.tensor_tensor(
+            out=table[:],
+            in0=row[:].unsqueeze(2).to_broadcast([P, PACK, DL, 16]),
+            in1=own_d[:].unsqueeze(1).unsqueeze(3).to_broadcast([P, PACK, DL, 16]),
+            op=ALU.mult,
+        )
+        x_row = keep.tile([P, 16], F32)
+        nc.vector.memset(x_row[:], 0.0)
+        nc.vector.memset(x_row[:, 0:3], 1.0)
+        nc.vector.memset(x_row[:, 3:6], -1.0)
+        nc.vector.tensor_scalar(out=x_row[:], in0=x_row[:], scalar1=first[:], scalar2=None, op0=ALU.mult)
+        x_table = keep.tile([P, DL, 16], BF16)
+        nc.vector.tensor_tensor(
+            out=x_table[:],
+            in0=x_row[:].unsqueeze(1).to_broadcast([P, DL, 16]),
+            in1=own_d[:].unsqueeze(2).to_broadcast([P, DL, 16]),
+            op=ALU.mult,
+        )
+        count_i = keep.tile([P, JQ], I32)
+        nc.gpsimd.iota(count_i[:], pattern=[[1, JQ]], base=0, channel_multiplier=0)
+        count = keep.tile([P, JQ], BF16)
+        nc.vector.tensor_copy(out=count[:], in_=count_i[:])
+
+        x_wide = keep.tile([P, D, JQ], BF16)
+        x_rep = keep.tile([P, PASSES, P], BF16)
+        above = keep.tile([P, PACK, PASSES, P], BF16)
+        got = keep.tile([P, 16, D], F32)
+        dist = keep.tile([P, 6, D], F32)
+        span3 = keep.tile([P, 3, D], F32)
+        span2 = keep.tile([P, 2, D], F32)
+        span1 = keep.tile([P, 1, D], F32)
+        pair = keep.tile([P, 2, D], F32)
+        denom = keep.tile([P, 4, D], F32)
+        inv = keep.tile([P, 4, D], F32)
+        mono = keep.tile([P, 4, D], F32)
+        left = keep.tile([P, 3, D], F32)
+        right = keep.tile([P, 3, D], F32)
+        values = keep.tile([P, 7, D], BF16)
+        turn = keep.tile([P, 4, D], BF16)
+        slot_v = keep.tile([P, 4, D], BF16)
+        slot_t = keep.tile([P, 4, D], BF16)
+        v_twice = keep.tile([P, PASSES * PACK * DL, 2], BF16)
+        q_twice = keep.tile([P, PASSES * PACK * DL, 2], BF16)
+        y_codes = keep.tile([P, PASSES, P], U32, align_bytes=64)
+        y_planes = keep.tile([P, PASSES, P], U8, align_bytes=64)
+
+        def planes(ap, n):
+            return ap.unsqueeze(1).to_broadcast([P, n, D])
+
+        for h in range(HALVES):
+            xh = x_sb[h]
+            nc.vector.tensor_copy(out=x_wide[:], in_=xh[:].unsqueeze(2).to_broadcast([P, D, JQ]))
+            x_wide_flat = x_wide[:].rearrange("p d j -> p (d j)")
+            for a in range(2):
+                xt = psum_fe.tile([P, 8, P], BF16, tag="fe")
+                for gi in range(8):
+                    g = 8 * a + gi
+                    nc.tensor.transpose(out=xt[:, gi, :], in_=x_wide_flat[:, g * P : (g + 1) * P], identity=ident[:])
+                nc.scalar.copy(out=x_rep[:, 8 * a : 8 * a + 8, :], in_=xt[:])
+            for tt in range(PACK):
+                nc.vector.tensor_scalar(
+                    out=above[:, tt], in0=x_rep[:], scalar1=wn[:, 4 + tt : 5 + tt], scalar2=None, op0=ALU.is_ge
+                )
+            for a in range(4):
+                gp = psum_fe.tile([P, 4, P], F32, tag="fe")
+                for gi in range(4):
+                    g = 4 * a + gi
+                    for tt in range(PACK):
+                        nc.tensor.matmul(
+                            out=gp[:, gi, :],
+                            lhsT=above[:, tt, g, :],
+                            rhs=table[:, tt].rearrange("p a f -> p (a f)"),
+                            start=(tt == 0),
+                            stop=False,
+                        )
+                    nc.tensor.matmul(
+                        out=gp[:, gi, :],
+                        lhsT=x_rep[:, g, :],
+                        rhs=x_table[:].rearrange("p a f -> p (a f)"),
+                        start=False,
+                        stop=True,
+                    )
+                nc.scalar.copy(
+                    out=got[:, :, 32 * a : 32 * a + 32].rearrange("p f (g a) -> p f g a", a=DL),
+                    in_=gp[:].rearrange("p g (a f) -> p f g a", f=16),
+                )
+            nc.vector.tensor_tensor(out=dist[:], in0=got[:, 0:6, :], in1=got[:, 6:12, :], op=ALU.add)
+            nc.vector.tensor_tensor(out=span3[:], in0=dist[:, 3:6, :], in1=dist[:, 0:3, :], op=ALU.add)
+            nc.vector.tensor_tensor(out=span2[:], in0=dist[:, 3:5, :], in1=dist[:, 1:3, :], op=ALU.add)
+            nc.vector.tensor_tensor(out=span1[:], in0=dist[:, 3:4, :], in1=dist[:, 2:3, :], op=ALU.add)
+            nc.vector.tensor_tensor(out=pair[:], in0=span2[:], in1=planes(span1[:, 0, :], 2), op=ALU.mult)
+            nc.vector.tensor_tensor(out=denom[:, 0:2, :], in0=span3[:, 0:2, :], in1=planes(pair[:, 0, :], 2), op=ALU.mult)
+            nc.vector.tensor_tensor(out=denom[:, 2, :], in0=span3[:, 2, :], in1=pair[:, 1, :], op=ALU.mult)
+            nc.vector.tensor_tensor(out=denom[:, 3, :], in0=span3[:, 1, :], in1=pair[:, 1, :], op=ALU.mult)
+            nc.vector.reciprocal(out=inv[:], in_=denom[:])
+            nc.scalar.square(out=mono[:, 0, :], in_=dist[:, 3, :])
+            nc.scalar.square(out=mono[:, 2, :], in_=dist[:, 2, :])
+            nc.vector.tensor_tensor(out=mono[:, 1:4:2, :], in0=dist[:, 1:3, :], in1=dist[:, 3:5, :], op=ALU.mult)
+            nc.vector.tensor_tensor(out=mono[:], in0=mono[:], in1=inv[:], op=ALU.mult)
+            nc.vector.tensor_tensor(out=mono[:, 1, :], in0=mono[:, 1, :], in1=mono[:, 3, :], op=ALU.add)
+            nc.vector.tensor_tensor(out=left[:], in0=mono[:, 0:3, :], in1=dist[:, 0:3, :], op=ALU.mult)
+            nc.vector.tensor_tensor(out=right[:], in0=mono[:, 0:3, :], in1=dist[:, 3:6, :], op=ALU.mult)
+            nc.vector.tensor_tensor(out=values[:, 1:3, :], in0=left[:, 0:2, :], in1=right[:, 1:3, :], op=ALU.add)
+            nc.vector.tensor_tensor(out=values[:, 5:7, :], in0=left[:, 0:2, :], in1=right[:, 1:3, :], op=ALU.add)
+            nc.scalar.copy(out=values[:, 0, :], in_=right[:, 0, :])
+            nc.scalar.copy(out=values[:, 4, :], in_=right[:, 0, :])
+            nc.scalar.copy(out=values[:, 3, :], in_=left[:, 2, :])
+            nc.vector.tensor_tensor(out=turn[:, 0:3, :], in0=got[:, 12:15, :], in1=got[:, 13:16, :], op=ALU.subtract)
+            nc.vector.scalar_tensor_tensor(
+                out=turn[:, 3, :], in0=got[:, 15, :], scalar=1.0, in1=got[:, 12, :], op0=ALU.add, op1=ALU.subtract
+            )
+            nc.vector.tensor_tensor(out=slot_v[:], in0=values[:, 3:7, :], in1=planes(turn[:, 0, :], 4), op=ALU.mult)
+            for c in range(1, 4):
+                nc.vector.tensor_tensor(
+                    out=slot_t[:], in0=values[:, 3 - c : 7 - c, :], in1=planes(turn[:, c, :], 4), op=ALU.mult
+                )
+                nc.vector.tensor_tensor(out=slot_v[:], in0=slot_v[:], in1=slot_t[:], op=ALU.add)
+            for tt in range(PACK):
+                nc.scalar.copy(
+                    out=v_twice[:].rearrange("p (g a b) r -> p g a b r", a=PACK, b=DL)[:, :, tt],
+                    in_=slot_v[:, tt, :].rearrange("p (g b) -> p g b", b=DL).unsqueeze(3).to_broadcast([P, PASSES, DL, 2]),
+                )
+                nc.scalar.copy(
+                    out=q_twice[:].rearrange("p (g a b) r -> p g a b r", a=PACK, b=DL)[:, :, tt],
+                    in_=got[:, 12 + tt, :].rearrange("p (g b) -> p g b", b=DL).unsqueeze(3).to_broadcast([P, PASSES, DL, 2]),
+                )
+
+            acc = []
+            for nu in range(N_TILES):
+                acc_nu = psum_acc.tile([P, N_TILE], F32, name="acc%d" % nu)
+                acc.append(acc_nu)
+            rows = CHUNK * PACK * DL
+            for kc in range(PASSES // CHUNK):
+                y_rows = work.tile([P, rows, JQ], BF16)
+                y_view = y_rows[:].rearrange("p c (j r) -> p c j r", r=2)
+                nc.vector.tensor_tensor(
+                    out=y_view,
+                    in0=q_twice[:, kc * rows : (kc + 1) * rows, :].unsqueeze(2).to_broadcast([P, rows, JQ // 2, 2]),
+                    in1=count[:].rearrange("p (j r) -> p j r", r=2).unsqueeze(1).to_broadcast([P, rows, JQ // 2, 2]),
+                    op=ALU.is_equal,
+                )
+                nc.vector.tensor_tensor(
+                    out=y_view,
+                    in0=y_view,
+                    in1=v_twice[:, kc * rows : (kc + 1) * rows, :].unsqueeze(2).to_broadcast([P, rows, JQ // 2, 2]),
+                    op=ALU.mult,
+                )
+                nc.scalar.activation(
+                    out=y_rows[:].rearrange("p (g a b) j -> p g a b j", a=PACK, b=DL)[:, :, PACK - 1, :, JQ - 1],
+                    in_=xh[:, kc * CHUNK * DL : (kc + 1) * CHUNK * DL].rearrange("p (g b) -> p g b", b=DL),
+                    func=ACT.Silu,
+                )
+                y_flat = y_rows[:].rearrange("p c j -> p (c j)")
+                grouped = work.tile([P, CHUNK, P, PACK], BF16, align_bytes=64)
+                for b in range(CHUNK // 2):
+                    yt = psum_fe.tile([P, 2, PACK, P], BF16, tag="fe")
+                    for gi in range(2):
+                        for tt in range(PACK):
+                            col = ((2 * b + gi) * PACK + tt) * P
+                            nc.tensor.transpose(out=yt[:, gi, tt, :], in_=y_flat[:, col : col + P], identity=ident[:])
+                    nc.scalar.copy(out=grouped[:, 2 * b : 2 * b + 2], in_=yt[:].rearrange("p g a m -> p g m a"))
+                g0 = kc * CHUNK
+                nc.vector.quantize_mx(
+                    out=y_codes[:, g0 : g0 + CHUNK, :].rearrange("p g m -> p (g m)").bitcast(FP8X4),
+                    scales=y_planes[:, g0 : g0 + CHUNK, :].rearrange("p g m -> p (g m)"),
+                    in_=grouped[:].rearrange("p g m a -> p (g m a)"),
+                )
+                for g in range(g0, g0 + CHUNK):
+                    for nu in range(N_TILES):
+                        cols = slice(nu * N_TILE, (nu + 1) * N_TILE)
+                        nc.tensor.matmul_mx(
+                            out=acc[nu][:],
+                            lhsT=y_codes[:, g, :].bitcast(FP8X4),
+                            lhsT_scale=y_planes[:, g, :],
+                            rhs=w_codes[g][:, cols].bitcast(FP8X4),
+                            rhs_scale=w_planes[4 * (g % 4) : P, g // 4, cols],
+                            start=(g == 0),
+                            stop=(g == PASSES - 1),
+                        )
+            for nu in range(N_TILES):
+                result = work.tile([P, N_TILE], F32)
+                nc.scalar.copy(out=result[:], in_=acc[nu][:])
+                nc.sync.dma_start(out=out[h * P : (h + 1) * P, nu * N_TILE : (nu + 1) * N_TILE], in_=result[:])

@@ -24,6 +24,8 @@ JQ = 16
 PACK = 4
 N_TILE = 512
 N_TILES = N // N_TILE
+UNIT = 8
+DU = UNIT * DL
 CHUNK = 4
 FLOPS = 2 * BATCH * D * 64 * N
 
@@ -33,9 +35,12 @@ def tile_regular_kan_w_kernel(tc, x, w_words, w_scales, t, k, out):
     assert k == 4
     with ExitStack() as ctx:
         keep = ctx.enter_context(tc.tile_pool(name="keep", bufs=1))
-        work = ctx.enter_context(tc.tile_pool(name="work", bufs=2))
+        temp = ctx.enter_context(tc.tile_pool(name="temp", bufs=1))
+        two_bufs = ctx.enter_context(tc.tile_pool(name="two_bufs", bufs=2))
+        four_bufs = ctx.enter_context(tc.tile_pool(name="four_bufs", bufs=4))
         psum_acc = ctx.enter_context(tc.psum_pool(name="acc", bufs=1))
         psum_fe = ctx.enter_context(tc.psum_pool(name="fe", bufs=4))
+        ctx.enter_context(tc.manual_schedule())
 
         knots16 = keep.tile([P, 4, 16], BF16)
         nc.vector.memset(knots16[:], 0.0)
@@ -68,16 +73,11 @@ def tile_regular_kan_w_kernel(tc, x, w_words, w_scales, t, k, out):
 
         ident = keep.tile([P, P], BF16)
         make_identity(nc, ident[:])
+        count_i = keep.tile([P, JQ], I32)
+        nc.gpsimd.iota(count_i[:], pattern=[[1, JQ]], base=0, channel_multiplier=0)
         ident_dj = ident[:].rearrange("p (a b) -> p a b", b=JQ)
         sel = keep.tile([P, DL, JQ], BF16)
         nc.vector.tensor_copy(out=sel[:], in_=ident[:, 0:JQ].unsqueeze(1).to_broadcast([P, DL, JQ]))
-        own_d = keep.tile([P, DL], F32)
-        nc.vector.tensor_reduce(out=own_d[:], in_=ident_dj, axis=AX.X, op=ALU.add)
-        first = keep.tile([P, 1], F32)
-        nc.vector.tensor_reduce(out=first[:], in_=ident_dj[:, :, 0], axis=AX.X, op=ALU.add)
-        later = keep.tile([P, 1], F32)
-        nc.vector.tensor_scalar(out=later[:], in0=first[:], scalar1=-1.0, scalar2=1.0, op0=ALU.mult, op1=ALU.add)
-
         rep_ps = psum_fe.tile([P, 64], F32, tag="fe")
         nc.tensor.matmul(
             out=rep_ps[:],
@@ -86,6 +86,36 @@ def tile_regular_kan_w_kernel(tc, x, w_words, w_scales, t, k, out):
             start=True,
             stop=True,
         )
+        own_d = keep.tile([P, DL], F32)
+        nc.vector.tensor_reduce(out=own_d[:], in_=ident_dj, axis=AX.X, op=ALU.add)
+        first = keep.tile([P, 1], F32)
+        nc.vector.tensor_reduce(out=first[:], in_=ident_dj[:, :, 0], axis=AX.X, op=ALU.add)
+        later = keep.tile([P, 1], F32)
+        nc.vector.tensor_scalar(out=later[:], in0=first[:], scalar1=-1.0, scalar2=1.0, op0=ALU.mult, op1=ALU.add)
+        sign = keep.tile([P, PACK, 6], F32)
+        nc.vector.memset(sign[:, :, 0:3], -1.0)
+        nc.vector.memset(sign[:, :, 3:6], 1.0)
+        nc.vector.tensor_scalar(out=sign[:, 0:3, :], in0=sign[:, 0:3, :], scalar1=later[:], scalar2=None, op0=ALU.mult)
+        x_row = keep.tile([P, 16], F32)
+        nc.vector.memset(x_row[:], 0.0)
+        nc.vector.memset(x_row[:, 0:3], 1.0)
+        nc.vector.memset(x_row[:, 3:6], -1.0)
+        nc.vector.tensor_scalar(out=x_row[:], in0=x_row[:], scalar1=first[:], scalar2=None, op0=ALU.mult)
+        x_table = keep.tile([P, DL, 16], BF16)
+        nc.vector.tensor_tensor(
+            out=x_table[:],
+            in0=x_row[:].unsqueeze(1).to_broadcast([P, DL, 16]),
+            in1=own_d[:].unsqueeze(2).to_broadcast([P, DL, 16]),
+            op=ALU.mult,
+        )
+        count = keep.tile([P, JQ], BF16)
+        nc.vector.tensor_copy(out=count[:], in_=count_i[:])
+        row = keep.tile([P, PACK, 16], BF16)
+        nc.vector.memset(row[:], 0.0)
+        nc.vector.tensor_copy(
+            out=row[:].rearrange("p a f -> p (a f)")[:, 12:64:17], in_=later[:].to_broadcast([P, PACK])
+        )
+
         wn = keep.tile([P, 12], F32)
         nc.vector.tensor_copy(
             out=wn[:].rearrange("p (a c) -> p a c", c=4),
@@ -99,19 +129,13 @@ def tile_regular_kan_w_kernel(tc, x, w_words, w_scales, t, k, out):
         nc.vector.tensor_copy(out=step_hi[:], in_=step[:])
         step_lo = keep.tile([P, 9], F32)
         nc.vector.tensor_tensor(out=step_lo[:], in0=step[:], in1=step_hi[:], op=ALU.subtract)
-
-        sign = keep.tile([P, PACK, 6], F32)
-        nc.vector.memset(sign[:, :, 0:3], -1.0)
-        nc.vector.memset(sign[:, :, 3:6], 1.0)
-        nc.vector.tensor_scalar(out=sign[:, 0:3, :], in0=sign[:, 0:3, :], scalar1=later[:], scalar2=None, op0=ALU.mult)
-        row = keep.tile([P, PACK, 16], BF16)
-        nc.vector.memset(row[:], 0.0)
+        rising = keep.tile([P, PACK, 2, 6], F32)
         for tt in range(PACK):
-            nc.vector.tensor_tensor(out=row[:, tt, 0:6], in0=step_hi[:, tt : tt + 6], in1=sign[:, tt, :], op=ALU.mult)
-            nc.vector.tensor_tensor(out=row[:, tt, 6:12], in0=step_lo[:, tt : tt + 6], in1=sign[:, tt, :], op=ALU.mult)
-        nc.vector.tensor_copy(
-            out=row[:].rearrange("p a f -> p (a f)")[:, 12:64:17], in_=later[:].to_broadcast([P, PACK])
-        )
+            nc.vector.tensor_tensor(out=rising[:, tt, 0, :], in0=step_hi[:, tt : tt + 6], in1=sign[:, tt, :], op=ALU.mult)
+            nc.vector.tensor_tensor(out=rising[:, tt, 1, :], in0=step_lo[:, tt : tt + 6], in1=sign[:, tt, :], op=ALU.mult)
+        row_knots = row[:, :, 0:12].rearrange("p a (b f) -> p a b f", f=6)
+        for f in range(6):
+            nc.vector.tensor_copy(out=row_knots[:, :, :, f], in_=rising[:, :, :, 3 * (f // 3) + 2 - f % 3])
         table = keep.tile([P, PACK, DL, 16], BF16)
         nc.vector.tensor_tensor(
             out=table[:],
@@ -119,180 +143,284 @@ def tile_regular_kan_w_kernel(tc, x, w_words, w_scales, t, k, out):
             in1=own_d[:].unsqueeze(1).unsqueeze(3).to_broadcast([P, PACK, DL, 16]),
             op=ALU.mult,
         )
-        x_row = keep.tile([P, 16], F32)
-        nc.vector.memset(x_row[:], 0.0)
-        nc.vector.memset(x_row[:, 0:3], 1.0)
-        nc.vector.memset(x_row[:, 3:6], -1.0)
-        nc.vector.tensor_scalar(out=x_row[:], in0=x_row[:], scalar1=first[:], scalar2=None, op0=ALU.mult)
-        x_table = keep.tile([P, DL, 16], BF16)
-        nc.vector.tensor_tensor(
-            out=x_table[:],
-            in0=x_row[:].unsqueeze(1).to_broadcast([P, DL, 16]),
-            in1=own_d[:].unsqueeze(2).to_broadcast([P, DL, 16]),
-            op=ALU.mult,
-        )
-        count_i = keep.tile([P, JQ], I32)
-        nc.gpsimd.iota(count_i[:], pattern=[[1, JQ]], base=0, channel_multiplier=0)
-        count = keep.tile([P, JQ], BF16)
-        nc.vector.tensor_copy(out=count[:], in_=count_i[:])
 
-        x_wide = keep.tile([P, D, JQ], BF16)
-        x_rep = keep.tile([P, PASSES, P], BF16)
-        above = keep.tile([P, PACK, PASSES, P], BF16)
-        got = keep.tile([P, 16, D], F32)
-        dist = keep.tile([P, 6, D], F32)
-        span3 = keep.tile([P, 3, D], F32)
-        span2 = keep.tile([P, 2, D], F32)
-        span1 = keep.tile([P, 1, D], F32)
-        pair = keep.tile([P, 2, D], F32)
-        denom = keep.tile([P, 4, D], F32)
-        inv = keep.tile([P, 4, D], F32)
-        mono = keep.tile([P, 4, D], F32)
-        left = keep.tile([P, 3, D], F32)
-        right = keep.tile([P, 3, D], F32)
-        values = keep.tile([P, 7, D], BF16)
-        turn = keep.tile([P, 4, D], BF16)
-        slot_v = keep.tile([P, 4, D], BF16)
-        slot_t = keep.tile([P, 4, D], BF16)
-        v_twice = keep.tile([P, PASSES * PACK * DL, 2], BF16)
-        q_twice = keep.tile([P, PASSES * PACK * DL, 2], BF16)
         y_codes = keep.tile([P, PASSES, P], U32, align_bytes=64)
         y_planes = keep.tile([P, PASSES, P], U8, align_bytes=64)
 
-        def planes(ap, n):
-            return ap.unsqueeze(1).to_broadcast([P, n, D])
+        units_per_half = PASSES // UNIT
+        x_wide, x_rep, above, got, q_twice, v_twice = {}, {}, {}, {}, {}, {}
+        dist, inv, turn = {}, {}, {}
 
-        for h in range(HALVES):
-            xh = x_sb[h]
-            nc.vector.tensor_copy(out=x_wide[:], in_=xh[:].unsqueeze(2).to_broadcast([P, D, JQ]))
-            x_wide_flat = x_wide[:].rearrange("p d j -> p (d j)")
-            for a in range(2):
-                xt = psum_fe.tile([P, 8, P], BF16, tag="fe")
-                for gi in range(8):
-                    g = 8 * a + gi
-                    nc.tensor.transpose(out=xt[:, gi, :], in_=x_wide_flat[:, g * P : (g + 1) * P], identity=ident[:])
-                nc.scalar.copy(out=x_rep[:, 8 * a : 8 * a + 8, :], in_=xt[:])
-            for tt in range(PACK):
-                nc.vector.tensor_scalar(
-                    out=above[:, tt], in0=x_rep[:], scalar1=wn[:, 4 + tt : 5 + tt], scalar2=None, op0=ALU.is_ge
-                )
-            for a in range(4):
+        def planes(ap, n):
+            return ap.unsqueeze(1).to_broadcast([P, n, DU])
+
+        def x_of(U):
+            u = U % units_per_half
+            return x_sb[U // units_per_half][:, u * DU : (u + 1) * DU]
+
+        def by_pass_and_byte(twice):
+            return twice[:].rearrange("p (g a b) r -> p g a b r", a=PACK, b=DL)
+
+        def twice_over(plane):
+            return plane.rearrange("p (g b) -> p g b", b=DL).unsqueeze(3).to_broadcast([P, UNIT, DL, 2])
+
+        def tt(out_ap, in0, in1, op):
+            return lambda: nc.vector.tensor_tensor(out=out_ap, in0=in0, in1=in1, op=op)
+
+        def take_turns(one, other):
+            merged = []
+            for i in range(max(len(one), len(other))):
+                merged.extend(one[i : i + 1])
+                merged.extend(other[i : i + 1])
+            return merged
+
+        def run(chain):
+            for instruction in chain:
+                instruction()
+
+        def widen(U):
+            wide = two_bufs.tile([P, DU, JQ], BF16, tag="rows")
+            nc.scalar.copy(out=wide[:], in_=x_of(U).unsqueeze(2).to_broadcast([P, DU, JQ]))
+            x_wide[U] = wide
+
+        def turn_x(U):
+            flat = x_wide[U][:].rearrange("p d j -> p (d j)")
+            rep = four_bufs.tile([P, UNIT, P], BF16, tag="x_rep")
+            xt = psum_fe.tile([P, UNIT, P], BF16, tag="fe")
+            for g in range(UNIT):
+                nc.tensor.transpose(out=xt[:, g, :], in_=flat[:, g * P : (g + 1) * P], identity=ident[:])
+            nc.scalar.copy(out=rep[:], in_=xt[:])
+            x_rep[U] = rep
+
+        def step_plane(ab, U, a):
+            return lambda: nc.vector.tensor_scalar(
+                out=ab[:, a], in0=x_rep[U][:], scalar1=wn[:, 4 + a : 5 + a], scalar2=None, op0=ALU.is_ge
+            )
+
+        def steps(U):
+            ab = two_bufs.tile([P, PACK, UNIT, P], BF16, tag="above")
+            above[U] = ab
+            return [step_plane(ab, U, a) for a in range(PACK)]
+
+        def sums(U):
+            gt = four_bufs.tile([P, 16, DU], F32, tag="got")
+            for a in range(UNIT // 4):
                 gp = psum_fe.tile([P, 4, P], F32, tag="fe")
                 for gi in range(4):
                     g = 4 * a + gi
-                    for tt in range(PACK):
+                    for b in range(PACK):
                         nc.tensor.matmul(
                             out=gp[:, gi, :],
-                            lhsT=above[:, tt, g, :],
-                            rhs=table[:, tt].rearrange("p a f -> p (a f)"),
-                            start=(tt == 0),
+                            lhsT=above[U][:, b, g, :],
+                            rhs=table[:, b].rearrange("p a f -> p (a f)"),
+                            start=(b == 0),
                             stop=False,
                         )
                     nc.tensor.matmul(
                         out=gp[:, gi, :],
-                        lhsT=x_rep[:, g, :],
+                        lhsT=x_rep[U][:, g, :],
                         rhs=x_table[:].rearrange("p a f -> p (a f)"),
                         start=False,
                         stop=True,
                     )
                 nc.scalar.copy(
-                    out=got[:, :, 32 * a : 32 * a + 32].rearrange("p f (g a) -> p f g a", a=DL),
+                    out=gt[:, :, 32 * a : 32 * a + 32].rearrange("p f (g a) -> p f g a", a=DL),
                     in_=gp[:].rearrange("p g (a f) -> p f g a", f=16),
                 )
-            nc.vector.tensor_tensor(out=dist[:], in0=got[:, 0:6, :], in1=got[:, 6:12, :], op=ALU.add)
-            nc.vector.tensor_tensor(out=span3[:], in0=dist[:, 3:6, :], in1=dist[:, 0:3, :], op=ALU.add)
-            nc.vector.tensor_tensor(out=span2[:], in0=dist[:, 3:5, :], in1=dist[:, 1:3, :], op=ALU.add)
-            nc.vector.tensor_tensor(out=span1[:], in0=dist[:, 3:4, :], in1=dist[:, 2:3, :], op=ALU.add)
-            nc.vector.tensor_tensor(out=pair[:], in0=span2[:], in1=planes(span1[:, 0, :], 2), op=ALU.mult)
-            nc.vector.tensor_tensor(out=denom[:, 0:2, :], in0=span3[:, 0:2, :], in1=planes(pair[:, 0, :], 2), op=ALU.mult)
-            nc.vector.tensor_tensor(out=denom[:, 2, :], in0=span3[:, 2, :], in1=pair[:, 1, :], op=ALU.mult)
-            nc.vector.tensor_tensor(out=denom[:, 3, :], in0=span3[:, 1, :], in1=pair[:, 1, :], op=ALU.mult)
-            nc.vector.reciprocal(out=inv[:], in_=denom[:])
-            nc.scalar.square(out=mono[:, 0, :], in_=dist[:, 3, :])
-            nc.scalar.square(out=mono[:, 2, :], in_=dist[:, 2, :])
-            nc.vector.tensor_tensor(out=mono[:, 1:4:2, :], in0=dist[:, 1:3, :], in1=dist[:, 3:5, :], op=ALU.mult)
-            nc.vector.tensor_tensor(out=mono[:], in0=mono[:], in1=inv[:], op=ALU.mult)
-            nc.vector.tensor_tensor(out=mono[:, 1, :], in0=mono[:, 1, :], in1=mono[:, 3, :], op=ALU.add)
-            nc.vector.tensor_tensor(out=left[:], in0=mono[:, 0:3, :], in1=dist[:, 0:3, :], op=ALU.mult)
-            nc.vector.tensor_tensor(out=right[:], in0=mono[:, 0:3, :], in1=dist[:, 3:6, :], op=ALU.mult)
-            nc.vector.tensor_tensor(out=values[:, 1:3, :], in0=left[:, 0:2, :], in1=right[:, 1:3, :], op=ALU.add)
-            nc.vector.tensor_tensor(out=values[:, 5:7, :], in0=left[:, 0:2, :], in1=right[:, 1:3, :], op=ALU.add)
-            nc.scalar.copy(out=values[:, 0, :], in_=right[:, 0, :])
-            nc.scalar.copy(out=values[:, 4, :], in_=right[:, 0, :])
-            nc.scalar.copy(out=values[:, 3, :], in_=left[:, 2, :])
-            nc.vector.tensor_tensor(out=turn[:, 0:3, :], in0=got[:, 12:15, :], in1=got[:, 13:16, :], op=ALU.subtract)
-            nc.vector.scalar_tensor_tensor(
-                out=turn[:, 3, :], in0=got[:, 15, :], scalar=1.0, in1=got[:, 12, :], op0=ALU.add, op1=ALU.subtract
-            )
-            nc.vector.tensor_tensor(out=slot_v[:], in0=values[:, 3:7, :], in1=planes(turn[:, 0, :], 4), op=ALU.mult)
-            for c in range(1, 4):
-                nc.vector.tensor_tensor(
-                    out=slot_t[:], in0=values[:, 3 - c : 7 - c, :], in1=planes(turn[:, c, :], 4), op=ALU.mult
-                )
-                nc.vector.tensor_tensor(out=slot_v[:], in0=slot_v[:], in1=slot_t[:], op=ALU.add)
-            for tt in range(PACK):
-                nc.scalar.copy(
-                    out=v_twice[:].rearrange("p (g a b) r -> p g a b r", a=PACK, b=DL)[:, :, tt],
-                    in_=slot_v[:, tt, :].rearrange("p (g b) -> p g b", b=DL).unsqueeze(3).to_broadcast([P, PASSES, DL, 2]),
-                )
-                nc.scalar.copy(
-                    out=q_twice[:].rearrange("p (g a b) r -> p g a b r", a=PACK, b=DL)[:, :, tt],
-                    in_=got[:, 12 + tt, :].rearrange("p (g b) -> p g b", b=DL).unsqueeze(3).to_broadcast([P, PASSES, DL, 2]),
-                )
+            qt = four_bufs.tile([P, UNIT * PACK * DL, 2], BF16, tag="q_twice")
+            for b in range(PACK):
+                nc.scalar.copy(out=by_pass_and_byte(qt)[:, :, b], in_=twice_over(gt[:, 12 + b, :]))
+            got[U] = gt
+            q_twice[U] = qt
 
-            acc = []
+        def spans(U):
+            gt = got[U]
+            ds = two_bufs.tile([P, 6, DU], F32, tag="dist")
+            tn = two_bufs.tile([P, 4, DU], BF16, tag="turn")
+            iv = two_bufs.tile([P, 4, DU], F32, tag="inv")
+            span3 = temp.tile([P, 3, DU], F32)
+            span2 = temp.tile([P, 2, DU], F32)
+            span1 = temp.tile([P, DU], F32)
+            pair = temp.tile([P, 2, DU], F32)
+            denom = temp.tile([P, 4, DU], F32)
+            two = temp.tile([P, 2, DU], F32)
+            four = temp.tile([P, DU], F32)
+            inv_four = temp.tile([P, DU], F32)
+            inv_two = temp.tile([P, 2, DU], F32)
+            dist[U], inv[U], turn[U] = ds, iv, tn
+            return [
+                tt(ds[:], gt[:, 0:6, :], gt[:, 6:12, :], ALU.add),
+                tt(tn[:, 0:3, :], gt[:, 12:15, :], gt[:, 13:16, :], ALU.subtract),
+                tt(span2[:], ds[:, 0:2, :], ds[:, 4:6, :], ALU.add),
+                tt(span1[:], ds[:, 0, :], ds[:, 5, :], ALU.add),
+                tt(span3[:], ds[:, 0:3, :], ds[:, 3:6, :], ALU.add),
+                tt(pair[:], span2[:], planes(span1[:], 2), ALU.mult),
+                lambda: nc.vector.scalar_tensor_tensor(
+                    out=tn[:, 3, :], in0=gt[:, 15, :], scalar=1.0, in1=gt[:, 12, :], op0=ALU.add, op1=ALU.subtract
+                ),
+                tt(denom[:, 0:2, :], span3[:, 0:2, :], planes(pair[:, 0, :], 2), ALU.mult),
+                tt(denom[:, 2, :], span3[:, 2, :], pair[:, 1, :], ALU.mult),
+                tt(denom[:, 3, :], span3[:, 1, :], pair[:, 1, :], ALU.mult),
+                tt(two[:], denom[:, 0:4:2, :], denom[:, 1:4:2, :], ALU.mult),
+                tt(four[:], two[:, 0, :], two[:, 1, :], ALU.mult),
+                lambda: nc.vector.reciprocal(out=inv_four[:], in_=four[:]),
+                tt(inv_two[:, 0, :], inv_four[:], two[:, 1, :], ALU.mult),
+                tt(inv_two[:, 1, :], inv_four[:], two[:, 0, :], ALU.mult),
+                tt(iv[:, 0:4:2, :], inv_two[:], denom[:, 1:4:2, :], ALU.mult),
+                tt(iv[:, 1:4:2, :], inv_two[:], denom[:, 0:4:2, :], ALU.mult),
+            ]
+
+        def cast(out_ap, in_ap):
+            return lambda: nc.vector.tensor_copy(out=out_ap, in_=in_ap)
+
+        def spread(vt, by_byte, b):
+            return lambda: nc.scalar.copy(
+                out=by_pass_and_byte(vt)[:, :, b], in_=twice_over(by_byte[:, PACK - 1 - b, :])
+            )
+
+        def values(U):
+            ds, iv, tn = dist[U], inv[U], turn[U]
+            mono = temp.tile([P, 4, DU], F32)
+            near = temp.tile([P, 3, DU], F32)
+            far = temp.tile([P, 3, DU], F32)
+            vals = temp.tile([P, 7, DU], BF16)
+            by_byte = temp.tile([P, 4, DU], BF16)
+            part1 = temp.tile([P, 4, DU], BF16)
+            part2 = temp.tile([P, 4, DU], BF16)
+            part3 = temp.tile([P, 4, DU], BF16)
+            vt = two_bufs.tile([P, UNIT * PACK * DL, 2], BF16, tag="v_twice")
+            v_twice[U] = vt
+            return [
+                tt(mono[:, 0:3:2, :], ds[:, 0:6:5, :], ds[:, 0:6:5, :], ALU.mult),
+                tt(mono[:, 1:4:2, :], ds[:, 0:2, :], ds[:, 4:6, :], ALU.mult),
+                tt(mono[:], mono[:], iv[:], ALU.mult),
+                tt(mono[:, 1, :], mono[:, 1, :], mono[:, 3, :], ALU.add),
+                tt(near[:], mono[:, 0:3, :], ds[:, 0:3, :], ALU.mult),
+                tt(far[:], mono[:, 0:3, :], ds[:, 3:6, :], ALU.mult),
+                cast(vals[:, 0, :], near[:, 0, :]),
+                tt(vals[:, 1:3, :], near[:, 1:3, :], far[:, 0:2, :], ALU.add),
+                cast(vals[:, 3, :], far[:, 2, :]),
+                cast(vals[:, 4:7, :], vals[:, 0:3, :]),
+                tt(by_byte[:], vals[:, 1:5, :], planes(tn[:, 0, :], 4), ALU.mult),
+                tt(part1[:], vals[:, 2:6, :], planes(tn[:, 1, :], 4), ALU.mult),
+                tt(part2[:], vals[:, 3:7, :], planes(tn[:, 2, :], 4), ALU.mult),
+                tt(part3[:], vals[:, 0:4, :], planes(tn[:, 3, :], 4), ALU.mult),
+                tt(by_byte[:], by_byte[:], part1[:], ALU.add),
+                tt(part2[:], part2[:], part3[:], ALU.add),
+                tt(by_byte[:], by_byte[:], part2[:], ALU.add),
+            ] + [spread(vt, by_byte, b) for b in range(PACK)]
+
+        rows = CHUNK * PACK * DL
+        chunks_per_unit = UNIT // CHUNK
+        chunks_per_half = PASSES // CHUNK
+        n_units = HALVES * units_per_half
+        assert chunks_per_unit == 2
+        y_rows, grouped, acc = {}, {}, {}
+
+        def first_pass(c):
+            return (c % chunks_per_half) * CHUNK
+
+        def expand(c):
+            U, kc = c // chunks_per_unit, c % chunks_per_unit
+            g0 = first_pass(c)
+            yr = two_bufs.tile([P, rows, JQ], BF16, tag="rows")
+            y_view = yr[:].rearrange("p c (j r) -> p c j r", r=2)
+            nc.vector.tensor_tensor(
+                out=y_view,
+                in0=q_twice[U][:, kc * rows : (kc + 1) * rows, :].unsqueeze(2).to_broadcast([P, rows, JQ // 2, 2]),
+                in1=count[:].rearrange("p (j r) -> p j r", r=2).unsqueeze(1).to_broadcast([P, rows, JQ // 2, 2]),
+                op=ALU.is_equal,
+            )
+            nc.vector.tensor_tensor(
+                out=y_view,
+                in0=y_view,
+                in1=v_twice[U][:, kc * rows : (kc + 1) * rows, :].unsqueeze(2).to_broadcast([P, rows, JQ // 2, 2]),
+                op=ALU.mult,
+            )
+            nc.scalar.activation(
+                out=yr[:].rearrange("p (g a b) j -> p g a b j", a=PACK, b=DL)[:, :, PACK - 1, :, JQ - 1],
+                in_=x_sb[c // chunks_per_half][:, g0 * DL : (g0 + CHUNK) * DL].rearrange("p (g b) -> p g b", b=DL),
+                func=ACT.Silu,
+            )
+            y_rows[c] = yr
+
+        def flip(c):
+            y_flat = y_rows[c][:].rearrange("p c j -> p (c j)")
+            gr = two_bufs.tile([P, CHUNK, P, PACK], BF16, tag="grouped", align_bytes=64)
+            for b in range(CHUNK // 2):
+                yt = psum_fe.tile([P, 2, PACK, P], BF16, tag="fe")
+                for gi in range(2):
+                    for tt in range(PACK):
+                        col = ((2 * b + gi) * PACK + tt) * P
+                        nc.tensor.transpose(out=yt[:, gi, tt, :], in_=y_flat[:, col : col + P], identity=ident[:])
+                nc.scalar.copy(out=gr[:, 2 * b : 2 * b + 2], in_=yt[:].rearrange("p g a m -> p g m a"))
+            grouped[c] = gr
+
+        def quantise(c):
+            g0 = first_pass(c)
+            nc.vector.quantize_mx(
+                out=y_codes[:, g0 : g0 + CHUNK, :].rearrange("p g m -> p (g m)").bitcast(FP8X4),
+                scales=y_planes[:, g0 : g0 + CHUNK, :].rearrange("p g m -> p (g m)"),
+                in_=grouped[c][:].rearrange("p g m a -> p (g m a)"),
+            )
+
+        def multiply(c):
+            h, g0 = c // chunks_per_half, first_pass(c)
+            if g0 == 0:
+                for nu in range(N_TILES):
+                    acc_nu = psum_acc.tile([P, N_TILE], F32, name="acc%d" % nu)
+                    acc[(h, nu)] = acc_nu
             for nu in range(N_TILES):
-                acc_nu = psum_acc.tile([P, N_TILE], F32, name="acc%d" % nu)
-                acc.append(acc_nu)
-            rows = CHUNK * PACK * DL
-            for kc in range(PASSES // CHUNK):
-                y_rows = work.tile([P, rows, JQ], BF16)
-                y_view = y_rows[:].rearrange("p c (j r) -> p c j r", r=2)
-                nc.vector.tensor_tensor(
-                    out=y_view,
-                    in0=q_twice[:, kc * rows : (kc + 1) * rows, :].unsqueeze(2).to_broadcast([P, rows, JQ // 2, 2]),
-                    in1=count[:].rearrange("p (j r) -> p j r", r=2).unsqueeze(1).to_broadcast([P, rows, JQ // 2, 2]),
-                    op=ALU.is_equal,
-                )
-                nc.vector.tensor_tensor(
-                    out=y_view,
-                    in0=y_view,
-                    in1=v_twice[:, kc * rows : (kc + 1) * rows, :].unsqueeze(2).to_broadcast([P, rows, JQ // 2, 2]),
-                    op=ALU.mult,
-                )
-                nc.scalar.activation(
-                    out=y_rows[:].rearrange("p (g a b) j -> p g a b j", a=PACK, b=DL)[:, :, PACK - 1, :, JQ - 1],
-                    in_=xh[:, kc * CHUNK * DL : (kc + 1) * CHUNK * DL].rearrange("p (g b) -> p g b", b=DL),
-                    func=ACT.Silu,
-                )
-                y_flat = y_rows[:].rearrange("p c j -> p (c j)")
-                grouped = work.tile([P, CHUNK, P, PACK], BF16, align_bytes=64)
-                for b in range(CHUNK // 2):
-                    yt = psum_fe.tile([P, 2, PACK, P], BF16, tag="fe")
-                    for gi in range(2):
-                        for tt in range(PACK):
-                            col = ((2 * b + gi) * PACK + tt) * P
-                            nc.tensor.transpose(out=yt[:, gi, tt, :], in_=y_flat[:, col : col + P], identity=ident[:])
-                    nc.scalar.copy(out=grouped[:, 2 * b : 2 * b + 2], in_=yt[:].rearrange("p g a m -> p g m a"))
-                g0 = kc * CHUNK
-                nc.vector.quantize_mx(
-                    out=y_codes[:, g0 : g0 + CHUNK, :].rearrange("p g m -> p (g m)").bitcast(FP8X4),
-                    scales=y_planes[:, g0 : g0 + CHUNK, :].rearrange("p g m -> p (g m)"),
-                    in_=grouped[:].rearrange("p g m a -> p (g m a)"),
-                )
+                cols = slice(nu * N_TILE, (nu + 1) * N_TILE)
                 for g in range(g0, g0 + CHUNK):
-                    for nu in range(N_TILES):
-                        cols = slice(nu * N_TILE, (nu + 1) * N_TILE)
-                        nc.tensor.matmul_mx(
-                            out=acc[nu][:],
-                            lhsT=y_codes[:, g, :].bitcast(FP8X4),
-                            lhsT_scale=y_planes[:, g, :],
-                            rhs=w_codes[g][:, cols].bitcast(FP8X4),
-                            rhs_scale=w_planes[4 * (g % 4) : P, g // 4, cols],
-                            start=(g == 0),
-                            stop=(g == PASSES - 1),
-                        )
+                    nc.tensor.matmul_mx(
+                        out=acc[(h, nu)][:],
+                        lhsT=y_codes[:, g, :].bitcast(FP8X4),
+                        lhsT_scale=y_planes[:, g, :],
+                        rhs=w_codes[g][:, cols].bitcast(FP8X4),
+                        rhs_scale=w_planes[4 * (g % 4) : P, g // 4, cols],
+                        start=(g == 0),
+                        stop=(g == PASSES - 1),
+                    )
+
+        def store(h):
             for nu in range(N_TILES):
-                result = work.tile([P, N_TILE], F32)
-                nc.scalar.copy(out=result[:], in_=acc[nu][:])
+                result = two_bufs.tile([P, N_TILE], F32, tag="result")
+                nc.scalar.copy(out=result[:], in_=acc[(h, nu)][:])
                 nc.sync.dma_start(out=out[h * P : (h + 1) * P, nu * N_TILE : (nu + 1) * N_TILE], in_=result[:])
+
+
+        widen(0)
+        for U in range(n_units):
+            if U + 1 < n_units:
+                widen(U + 1)
+            turn_x(U)
+        run(steps(0))
+        run(steps(1))
+        sums(0)
+        sums(1)
+        run(take_turns(spans(0), steps(2) + steps(3)))
+        sums(2)
+        sums(3)
+        run(take_turns(values(0), spans(1)))
+        for U in range(n_units):
+            c = U * chunks_per_unit
+            expand(c)
+            flip(c)
+            if c > 0:
+                multiply(c - 1)
+            expand(c + 1)
+            if c > 0 and c % chunks_per_half == 0:
+                store(c // chunks_per_half - 1)
+            flip(c + 1)
+            ahead = take_turns(
+                values(U + 1) if U + 1 < n_units else [],
+                spans(U + 2) if U + 2 < n_units else [],
+            )
+            run(ahead[: len(ahead) // 2])
+            quantise(c)
+            multiply(c)
+            run(ahead[len(ahead) // 2 :])
+            quantise(c + 1)
+        multiply(n_units * chunks_per_unit - 1)
+        store(HALVES - 1)

@@ -44,15 +44,20 @@ def tile_regular_kan_w_kernel(tc, x, w_words, w_scales, t, k, out):
 
         knots16 = keep.tile([P, 4, 16], BF16)
         nc.vector.memset(knots16[:], 0.0)
-        nc.sync.dma_start(out=knots16[1:16, 0, 0:4], in_=t[0:60].rearrange("(q c) -> q c", c=4))
-        nc.sync.dma_start(out=knots16[0:16, 1, 0:4], in_=t[0:64].rearrange("(q c) -> q c", c=4))
-        nc.sync.dma_start(out=knots16[0:15, 2, 0:4], in_=t[4:64].rearrange("(q c) -> q c", c=4))
-        nc.sync.dma_start(out=knots16[15:16, 2, 0:3], in_=t[64:67].rearrange("(o c) -> o c", o=1))
+        nc.scalar.dma_start(out=knots16[1:16, 0, 0:4], in_=t[0:60].rearrange("(q c) -> q c", c=4))
+        nc.scalar.dma_start(out=knots16[0:16, 1, 0:4], in_=t[0:64].rearrange("(q c) -> q c", c=4))
+        nc.scalar.dma_start(out=knots16[0:15, 2, 0:4], in_=t[4:64].rearrange("(q c) -> q c", c=4))
+        nc.scalar.dma_start(out=knots16[15:16, 2, 0:3], in_=t[64:67].rearrange("(o c) -> o c", o=1))
         x_sb = []
         for h in range(HALVES):
             x_half = keep.tile([P, D], BF16, name="x_half%d" % h)
             nc.sync.dma_start(out=x_half[:], in_=x[h * P : (h + 1) * P, :])
             x_sb.append(x_half)
+        silu_sb = []
+        for h in range(HALVES):
+            silu_half = keep.tile([P, D], BF16, name="silu_half%d" % h)
+            nc.scalar.activation(out=silu_half[:], in_=x_sb[h][:], func=ACT.Silu)
+            silu_sb.append(silu_half)
 
         w_planes = keep.tile([P, PASSES // 4, N], U8, align_bytes=64)
         nc.vector.memset(w_planes[:].rearrange("p s n -> p (s n)").bitcast(I32), 0)
@@ -117,33 +122,7 @@ def tile_regular_kan_w_kernel(tc, x, w_words, w_scales, t, k, out):
         )
 
         wn = keep.tile([P, 12], F32)
-        nc.vector.tensor_copy(
-            out=wn[:].rearrange("p (a c) -> p a c", c=4),
-            in_=rep_ps[:].rearrange("p (a c) -> p a c", c=16)[:, 0:3, 0:4],
-        )
-        prev = keep.tile([P, 9], F32)
-        nc.vector.tensor_scalar(out=prev[:], in0=wn[:, 1:10], scalar1=later[:], scalar2=None, op0=ALU.mult)
-        step = keep.tile([P, 9], F32)
-        nc.vector.tensor_tensor(out=step[:], in0=wn[:, 2:11], in1=prev[:], op=ALU.subtract)
-        step_hi = keep.tile([P, 9], BF16)
-        nc.vector.tensor_copy(out=step_hi[:], in_=step[:])
-        step_lo = keep.tile([P, 9], F32)
-        nc.vector.tensor_tensor(out=step_lo[:], in0=step[:], in1=step_hi[:], op=ALU.subtract)
-        rising = keep.tile([P, PACK, 2, 6], F32)
-        for tt in range(PACK):
-            nc.vector.tensor_tensor(out=rising[:, tt, 0, :], in0=step_hi[:, tt : tt + 6], in1=sign[:, tt, :], op=ALU.mult)
-            nc.vector.tensor_tensor(out=rising[:, tt, 1, :], in0=step_lo[:, tt : tt + 6], in1=sign[:, tt, :], op=ALU.mult)
-        row_knots = row[:, :, 0:12].rearrange("p a (b f) -> p a b f", f=6)
-        for f in range(6):
-            nc.vector.tensor_copy(out=row_knots[:, :, :, f], in_=rising[:, :, :, 3 * (f // 3) + 2 - f % 3])
         table = keep.tile([P, PACK, DL, 16], BF16)
-        nc.vector.tensor_tensor(
-            out=table[:],
-            in0=row[:].unsqueeze(2).to_broadcast([P, PACK, DL, 16]),
-            in1=own_d[:].unsqueeze(1).unsqueeze(3).to_broadcast([P, PACK, DL, 16]),
-            op=ALU.mult,
-        )
-
         y_codes = keep.tile([P, PASSES, P], U32, align_bytes=64)
         y_planes = keep.tile([P, PASSES, P], U8, align_bytes=64)
 
@@ -167,6 +146,9 @@ def tile_regular_kan_w_kernel(tc, x, w_words, w_scales, t, k, out):
         def tt(out_ap, in0, in1, op):
             return lambda: nc.vector.tensor_tensor(out=out_ap, in0=in0, in1=in1, op=op)
 
+        def cast(out_ap, in_ap):
+            return lambda: nc.vector.tensor_copy(out=out_ap, in_=in_ap)
+
         def take_turns(one, other):
             merged = []
             for i in range(max(len(one), len(other))):
@@ -180,8 +162,8 @@ def tile_regular_kan_w_kernel(tc, x, w_words, w_scales, t, k, out):
 
         def widen(U):
             wide = two_bufs.tile([P, DU, JQ], BF16, tag="rows")
-            nc.scalar.copy(out=wide[:], in_=x_of(U).unsqueeze(2).to_broadcast([P, DU, JQ]))
             x_wide[U] = wide
+            return [cast(wide[:], x_of(U).unsqueeze(2).to_broadcast([P, DU, JQ]))]
 
         def turn_x(U):
             flat = x_wide[U][:].rearrange("p d j -> p (d j)")
@@ -227,10 +209,12 @@ def tile_regular_kan_w_kernel(tc, x, w_words, w_scales, t, k, out):
                     out=gt[:, :, 32 * a : 32 * a + 32].rearrange("p f (g a) -> p f g a", a=DL),
                     in_=gp[:].rearrange("p g (a f) -> p f g a", f=16),
                 )
+            got[U] = gt
+
+        def places(U):
             qt = four_bufs.tile([P, UNIT * PACK * DL, 2], BF16, tag="q_twice")
             for b in range(PACK):
-                nc.scalar.copy(out=by_pass_and_byte(qt)[:, :, b], in_=twice_over(gt[:, 12 + b, :]))
-            got[U] = gt
+                nc.scalar.copy(out=by_pass_and_byte(qt)[:, :, b], in_=twice_over(got[U][:, 12 + b, :]))
             q_twice[U] = qt
 
         def spans(U):
@@ -251,9 +235,9 @@ def tile_regular_kan_w_kernel(tc, x, w_words, w_scales, t, k, out):
             return [
                 tt(ds[:], gt[:, 0:6, :], gt[:, 6:12, :], ALU.add),
                 tt(tn[:, 0:3, :], gt[:, 12:15, :], gt[:, 13:16, :], ALU.subtract),
-                tt(span2[:], ds[:, 0:2, :], ds[:, 4:6, :], ALU.add),
-                tt(span1[:], ds[:, 0, :], ds[:, 5, :], ALU.add),
-                tt(span3[:], ds[:, 0:3, :], ds[:, 3:6, :], ALU.add),
+                tt(span2[:], ds[:, 3:5, :], ds[:, 1:3, :], ALU.add),
+                tt(span1[:], ds[:, 3, :], ds[:, 2, :], ALU.add),
+                tt(span3[:], ds[:, 3:6, :], ds[:, 0:3, :], ALU.add),
                 tt(pair[:], span2[:], planes(span1[:], 2), ALU.mult),
                 lambda: nc.vector.scalar_tensor_tensor(
                     out=tn[:, 3, :], in0=gt[:, 15, :], scalar=1.0, in1=gt[:, 12, :], op0=ALU.add, op1=ALU.subtract
@@ -270,20 +254,13 @@ def tile_regular_kan_w_kernel(tc, x, w_words, w_scales, t, k, out):
                 tt(iv[:, 1:4:2, :], inv_two[:], denom[:, 0:4:2, :], ALU.mult),
             ]
 
-        def cast(out_ap, in_ap):
-            return lambda: nc.vector.tensor_copy(out=out_ap, in_=in_ap)
-
-        def spread(vt, by_byte, b):
-            return lambda: nc.scalar.copy(
-                out=by_pass_and_byte(vt)[:, :, b], in_=twice_over(by_byte[:, PACK - 1 - b, :])
-            )
-
         def values(U):
             ds, iv, tn = dist[U], inv[U], turn[U]
             mono = temp.tile([P, 4, DU], F32)
-            near = temp.tile([P, 3, DU], F32)
-            far = temp.tile([P, 3, DU], F32)
-            vals = temp.tile([P, 7, DU], BF16)
+            left = temp.tile([P, 3, DU], F32)
+            right = temp.tile([P, 3, DU], F32)
+            vals = temp.tile([P, 8, DU], BF16)
+            both = vals[:].rearrange("p (r a) d -> p r a d", a=4)
             by_byte = temp.tile([P, 4, DU], BF16)
             part1 = temp.tile([P, 4, DU], BF16)
             part2 = temp.tile([P, 4, DU], BF16)
@@ -291,24 +268,68 @@ def tile_regular_kan_w_kernel(tc, x, w_words, w_scales, t, k, out):
             vt = two_bufs.tile([P, UNIT * PACK * DL, 2], BF16, tag="v_twice")
             v_twice[U] = vt
             return [
-                tt(mono[:, 0:3:2, :], ds[:, 0:6:5, :], ds[:, 0:6:5, :], ALU.mult),
-                tt(mono[:, 1:4:2, :], ds[:, 0:2, :], ds[:, 4:6, :], ALU.mult),
+                tt(mono[:, 1:4:2, :], ds[:, 1:3, :], ds[:, 3:5, :], ALU.mult),
+                tt(mono[:, 0, :], ds[:, 3, :], ds[:, 3, :], ALU.mult),
+                tt(mono[:, 2, :], ds[:, 2, :], ds[:, 2, :], ALU.mult),
                 tt(mono[:], mono[:], iv[:], ALU.mult),
                 tt(mono[:, 1, :], mono[:, 1, :], mono[:, 3, :], ALU.add),
-                tt(near[:], mono[:, 0:3, :], ds[:, 0:3, :], ALU.mult),
-                tt(far[:], mono[:, 0:3, :], ds[:, 3:6, :], ALU.mult),
-                cast(vals[:, 0, :], near[:, 0, :]),
-                tt(vals[:, 1:3, :], near[:, 1:3, :], far[:, 0:2, :], ALU.add),
-                cast(vals[:, 3, :], far[:, 2, :]),
-                cast(vals[:, 4:7, :], vals[:, 0:3, :]),
-                tt(by_byte[:], vals[:, 1:5, :], planes(tn[:, 0, :], 4), ALU.mult),
+                tt(left[:], mono[:, 0:3, :], ds[:, 0:3, :], ALU.mult),
+                tt(right[:], mono[:, 0:3, :], ds[:, 3:6, :], ALU.mult),
+                cast(both[:, :, 3, :], planes(left[:, 2, :], 2)),
+                tt(
+                    both[:, :, 1:3, :],
+                    left[:, 0:2, :].unsqueeze(1).to_broadcast([P, 2, 2, DU]),
+                    right[:, 1:3, :].unsqueeze(1).to_broadcast([P, 2, 2, DU]),
+                    ALU.add,
+                ),
+                cast(both[:, :, 0, :], planes(right[:, 0, :], 2)),
+                tt(by_byte[:], vals[:, 3:7, :], planes(tn[:, 0, :], 4), ALU.mult),
                 tt(part1[:], vals[:, 2:6, :], planes(tn[:, 1, :], 4), ALU.mult),
-                tt(part2[:], vals[:, 3:7, :], planes(tn[:, 2, :], 4), ALU.mult),
+                tt(part2[:], vals[:, 1:5, :], planes(tn[:, 2, :], 4), ALU.mult),
                 tt(part3[:], vals[:, 0:4, :], planes(tn[:, 3, :], 4), ALU.mult),
                 tt(by_byte[:], by_byte[:], part1[:], ALU.add),
                 tt(part2[:], part2[:], part3[:], ALU.add),
                 tt(by_byte[:], by_byte[:], part2[:], ALU.add),
-            ] + [spread(vt, by_byte, b) for b in range(PACK)]
+                cast(
+                    by_pass_and_byte(vt),
+                    by_byte[:].rearrange("p a (g b) -> p g a b", b=DL).unsqueeze(4).to_broadcast([P, UNIT, PACK, DL, 2]),
+                ),
+            ]
+
+        def knot_table():
+            prev = keep.tile([P, 9], F32)
+            step = keep.tile([P, 9], F32)
+            halves = keep.tile([P, 2, 9], BF16)
+            chain = [
+                cast(
+                    wn[:].rearrange("p (a c) -> p a c", c=4),
+                    rep_ps[:].rearrange("p (a c) -> p a c", c=16)[:, 0:3, 0:4],
+                ),
+                lambda: nc.vector.tensor_scalar(
+                    out=prev[:], in0=wn[:, 1:10], scalar1=later[:], scalar2=None, op0=ALU.mult
+                ),
+                tt(step[:], wn[:, 2:11], prev[:], ALU.subtract),
+                cast(halves[:, 0, :], step[:]),
+                tt(halves[:, 1, :], step[:], halves[:, 0, :], ALU.subtract),
+            ]
+            for a in range(PACK):
+                chain.append(
+                    tt(
+                        row[:, a, 0:12].rearrange("p (b f) -> p b f", f=6),
+                        halves[:, :, a : a + 6],
+                        sign[:, a, :].unsqueeze(1).to_broadcast([P, 2, 6]),
+                        ALU.mult,
+                    )
+                )
+            chain.append(
+                tt(
+                    table[:],
+                    row[:].unsqueeze(2).to_broadcast([P, PACK, DL, 16]),
+                    own_d[:].unsqueeze(1).unsqueeze(3).to_broadcast([P, PACK, DL, 16]),
+                    ALU.mult,
+                )
+            )
+            return chain
 
         rows = CHUNK * PACK * DL
         chunks_per_unit = UNIT // CHUNK
@@ -320,29 +341,32 @@ def tile_regular_kan_w_kernel(tc, x, w_words, w_scales, t, k, out):
         def first_pass(c):
             return (c % chunks_per_half) * CHUNK
 
-        def expand(c):
-            U, kc = c // chunks_per_unit, c % chunks_per_unit
-            g0 = first_pass(c)
-            yr = two_bufs.tile([P, rows, JQ], BF16, tag="rows")
-            y_view = yr[:].rearrange("p c (j r) -> p c j r", r=2)
-            nc.vector.tensor_tensor(
-                out=y_view,
-                in0=q_twice[U][:, kc * rows : (kc + 1) * rows, :].unsqueeze(2).to_broadcast([P, rows, JQ // 2, 2]),
-                in1=count[:].rearrange("p (j r) -> p j r", r=2).unsqueeze(1).to_broadcast([P, rows, JQ // 2, 2]),
-                op=ALU.is_equal,
-            )
-            nc.vector.tensor_tensor(
-                out=y_view,
-                in0=y_view,
-                in1=v_twice[U][:, kc * rows : (kc + 1) * rows, :].unsqueeze(2).to_broadcast([P, rows, JQ // 2, 2]),
-                op=ALU.mult,
-            )
-            nc.scalar.activation(
-                out=yr[:].rearrange("p (g a b) j -> p g a b j", a=PACK, b=DL)[:, :, PACK - 1, :, JQ - 1],
-                in_=x_sb[c // chunks_per_half][:, g0 * DL : (g0 + CHUNK) * DL].rearrange("p (g b) -> p g b", b=DL),
-                func=ACT.Silu,
-            )
-            y_rows[c] = yr
+        def expand(first, count_of):
+            chunks = range(first, first + count_of)
+            view, where, what = {}, {}, {}
+            for c in chunks:
+                U, kc = c // chunks_per_unit, c % chunks_per_unit
+                yr = two_bufs.tile([P, rows, JQ], BF16, tag="rows")
+                y_rows[c] = yr
+                view[c] = yr[:].rearrange("p c (j r) -> p c j r", r=2)
+                part = slice(kc * rows, (kc + 1) * rows)
+                where[c] = q_twice[U][:, part, :].unsqueeze(2).to_broadcast([P, rows, JQ // 2, 2])
+                what[c] = v_twice[U][:, part, :].unsqueeze(2).to_broadcast([P, rows, JQ // 2, 2])
+            for c in chunks:
+                nc.vector.tensor_tensor(
+                    out=view[c],
+                    in0=where[c],
+                    in1=count[:].rearrange("p (j r) -> p j r", r=2).unsqueeze(1).to_broadcast([P, rows, JQ // 2, 2]),
+                    op=ALU.is_equal,
+                )
+            for c in chunks:
+                nc.vector.tensor_tensor(out=view[c], in0=view[c], in1=what[c], op=ALU.mult)
+            for c in chunks:
+                g0 = first_pass(c)
+                nc.vector.tensor_copy(
+                    out=y_rows[c][:].rearrange("p (g a b) j -> p g a b j", a=PACK, b=DL)[:, :, PACK - 1, :, JQ - 1],
+                    in_=silu_sb[c // chunks_per_half][:, g0 * DL : (g0 + CHUNK) * DL].rearrange("p (g b) -> p g b", b=DL),
+                )
 
         def flip(c):
             y_flat = y_rows[c][:].rearrange("p c j -> p (c j)")
@@ -357,12 +381,13 @@ def tile_regular_kan_w_kernel(tc, x, w_words, w_scales, t, k, out):
             grouped[c] = gr
 
         def quantise(c):
-            g0 = first_pass(c)
-            nc.vector.quantize_mx(
-                out=y_codes[:, g0 : g0 + CHUNK, :].rearrange("p g m -> p (g m)").bitcast(FP8X4),
-                scales=y_planes[:, g0 : g0 + CHUNK, :].rearrange("p g m -> p (g m)"),
-                in_=grouped[c][:].rearrange("p g m a -> p (g m a)"),
-            )
+            for b in range(CHUNK // 2):
+                g0 = first_pass(c) + 2 * b
+                nc.vector.quantize_mx(
+                    out=y_codes[:, g0 : g0 + 2, :].rearrange("p g m -> p (g m)").bitcast(FP8X4),
+                    scales=y_planes[:, g0 : g0 + 2, :].rearrange("p g m -> p (g m)"),
+                    in_=grouped[c][:, 2 * b : 2 * b + 2].rearrange("p g m a -> p (g m a)"),
+                )
 
         def multiply(c):
             h, g0 = c // chunks_per_half, first_pass(c)
@@ -370,18 +395,19 @@ def tile_regular_kan_w_kernel(tc, x, w_words, w_scales, t, k, out):
                 for nu in range(N_TILES):
                     acc_nu = psum_acc.tile([P, N_TILE], F32, name="acc%d" % nu)
                     acc[(h, nu)] = acc_nu
-            for nu in range(N_TILES):
-                cols = slice(nu * N_TILE, (nu + 1) * N_TILE)
-                for g in range(g0, g0 + CHUNK):
-                    nc.tensor.matmul_mx(
-                        out=acc[(h, nu)][:],
-                        lhsT=y_codes[:, g, :].bitcast(FP8X4),
-                        lhsT_scale=y_planes[:, g, :],
-                        rhs=w_codes[g][:, cols].bitcast(FP8X4),
-                        rhs_scale=w_planes[4 * (g % 4) : P, g // 4, cols],
-                        start=(g == 0),
-                        stop=(g == PASSES - 1),
-                    )
+            for b in range(CHUNK // 2):
+                for nu in range(N_TILES):
+                    cols = slice(nu * N_TILE, (nu + 1) * N_TILE)
+                    for g in range(g0 + 2 * b, g0 + 2 * b + 2):
+                        nc.tensor.matmul_mx(
+                            out=acc[(h, nu)][:],
+                            lhsT=y_codes[:, g, :].bitcast(FP8X4),
+                            lhsT_scale=y_planes[:, g, :],
+                            rhs=w_codes[g][:, cols].bitcast(FP8X4),
+                            rhs_scale=w_planes[4 * (g % 4) : P, g // 4, cols],
+                            start=(g == 0),
+                            stop=(g == PASSES - 1),
+                        )
 
         def store(h):
             for nu in range(N_TILES):
@@ -390,29 +416,36 @@ def tile_regular_kan_w_kernel(tc, x, w_words, w_scales, t, k, out):
                 nc.sync.dma_start(out=out[h * P : (h + 1) * P, nu * N_TILE : (nu + 1) * N_TILE], in_=result[:])
 
 
-        widen(0)
-        for U in range(n_units):
-            if U + 1 < n_units:
-                widen(U + 1)
-            turn_x(U)
+        table_chain = knot_table()
+        cut = len(table_chain) // 2
+        run(take_turns(table_chain[:cut], widen(0) + widen(1)))
+        turn_x(0)
+        turn_x(1)
+        run(take_turns(table_chain[cut:], widen(2) + widen(3)))
+        turn_x(2)
+        turn_x(3)
         run(steps(0))
         run(steps(1))
         sums(0)
         sums(1)
         run(take_turns(spans(0), steps(2) + steps(3)))
+        places(0)
+        places(1)
         sums(2)
         sums(3)
         run(take_turns(values(0), spans(1)))
         for U in range(n_units):
             c = U * chunks_per_unit
-            expand(c)
+            expand(c, chunks_per_unit)
             flip(c)
             if c > 0:
+                quantise(c - 1)
                 multiply(c - 1)
-            expand(c + 1)
             if c > 0 and c % chunks_per_half == 0:
                 store(c // chunks_per_half - 1)
             flip(c + 1)
+            if U + 2 < n_units:
+                places(U + 2)
             ahead = take_turns(
                 values(U + 1) if U + 1 < n_units else [],
                 spans(U + 2) if U + 2 < n_units else [],
@@ -421,6 +454,6 @@ def tile_regular_kan_w_kernel(tc, x, w_words, w_scales, t, k, out):
             quantise(c)
             multiply(c)
             run(ahead[len(ahead) // 2 :])
-            quantise(c + 1)
+        quantise(n_units * chunks_per_unit - 1)
         multiply(n_units * chunks_per_unit - 1)
         store(HALVES - 1)

@@ -78,6 +78,8 @@ def tile_regular_kan_w_kernel(tc, x, w_words, w_scales, t, k, out):
 
         ident = keep.tile([P, P], BF16)
         make_identity(nc, ident[:])
+        ident_words = keep.tile([P, P], F32)
+        make_identity(nc, ident_words[:])
         count_i = keep.tile([P, JQ], I32)
         nc.gpsimd.iota(count_i[:], pattern=[[1, JQ]], base=0, channel_multiplier=0)
         ident_dj = ident[:].rearrange("p (a b) -> p a b", b=JQ)
@@ -113,8 +115,8 @@ def tile_regular_kan_w_kernel(tc, x, w_words, w_scales, t, k, out):
             in1=own_d[:].unsqueeze(2).to_broadcast([P, DL, 16]),
             op=ALU.mult,
         )
-        count = keep.tile([P, JQ], BF16)
-        nc.vector.tensor_copy(out=count[:], in_=count_i[:])
+        count = keep.tile([P, JQ, 2], BF16)
+        nc.vector.tensor_copy(out=count[:], in_=count_i[:].unsqueeze(2).to_broadcast([P, JQ, 2]))
         row = keep.tile([P, PACK, 16], BF16)
         nc.vector.memset(row[:], 0.0)
         nc.vector.tensor_copy(
@@ -138,10 +140,7 @@ def tile_regular_kan_w_kernel(tc, x, w_words, w_scales, t, k, out):
             return x_sb[U // units_per_half][:, u * DU : (u + 1) * DU]
 
         def by_pass_and_byte(twice):
-            return twice[:].rearrange("p (g a b) r -> p g a b r", a=PACK, b=DL)
-
-        def twice_over(plane):
-            return plane.rearrange("p (g b) -> p g b", b=DL).unsqueeze(3).to_broadcast([P, UNIT, DL, 2])
+            return twice[:].rearrange("p (g u b) e -> p g u b e", u=2, b=DL)
 
         def tt(out_ap, in0, in1, op):
             return lambda: nc.vector.tensor_tensor(out=out_ap, in0=in0, in1=in1, op=op)
@@ -212,9 +211,12 @@ def tile_regular_kan_w_kernel(tc, x, w_words, w_scales, t, k, out):
             got[U] = gt
 
         def places(U):
-            qt = four_bufs.tile([P, UNIT * PACK * DL, 2], BF16, tag="q_twice")
+            qt = four_bufs.tile([P, UNIT * 2 * DL, 2], BF16, tag="q_twice")
             for b in range(PACK):
-                nc.scalar.copy(out=by_pass_and_byte(qt)[:, :, b], in_=twice_over(got[U][:, 12 + b, :]))
+                nc.scalar.copy(
+                    out=by_pass_and_byte(qt)[:, :, b // 2, :, b % 2],
+                    in_=got[U][:, 12 + b, :].rearrange("p (g b) -> p g b", b=DL),
+                )
             q_twice[U] = qt
 
         def spans(U):
@@ -265,7 +267,7 @@ def tile_regular_kan_w_kernel(tc, x, w_words, w_scales, t, k, out):
             part1 = temp.tile([P, 4, DU], BF16)
             part2 = temp.tile([P, 4, DU], BF16)
             part3 = temp.tile([P, 4, DU], BF16)
-            vt = two_bufs.tile([P, UNIT * PACK * DL, 2], BF16, tag="v_twice")
+            vt = two_bufs.tile([P, UNIT * 2 * DL, 2], BF16, tag="v_twice")
             v_twice[U] = vt
             return [
                 tt(mono[:, 1:4:2, :], ds[:, 1:3, :], ds[:, 3:5, :], ALU.mult),
@@ -290,10 +292,7 @@ def tile_regular_kan_w_kernel(tc, x, w_words, w_scales, t, k, out):
                 tt(by_byte[:], by_byte[:], part1[:], ALU.add),
                 tt(part2[:], part2[:], part3[:], ALU.add),
                 tt(by_byte[:], by_byte[:], part2[:], ALU.add),
-                cast(
-                    by_pass_and_byte(vt),
-                    by_byte[:].rearrange("p a (g b) -> p g a b", b=DL).unsqueeze(4).to_broadcast([P, UNIT, PACK, DL, 2]),
-                ),
+                cast(by_pass_and_byte(vt), by_byte[:].rearrange("p (u e) (g b) -> p g u b e", e=2, b=DL)),
             ]
 
         def knot_table():
@@ -331,7 +330,7 @@ def tile_regular_kan_w_kernel(tc, x, w_words, w_scales, t, k, out):
             )
             return chain
 
-        rows = CHUNK * PACK * DL
+        rows = CHUNK * 2 * DL
         chunks_per_unit = UNIT // CHUNK
         chunks_per_half = PASSES // CHUNK
         n_units = HALVES * units_per_half
@@ -346,17 +345,17 @@ def tile_regular_kan_w_kernel(tc, x, w_words, w_scales, t, k, out):
             view, where, what = {}, {}, {}
             for c in chunks:
                 U, kc = c // chunks_per_unit, c % chunks_per_unit
-                yr = two_bufs.tile([P, rows, JQ], BF16, tag="rows")
+                yr = two_bufs.tile([P, rows, JQ, 2], BF16, tag="rows")
                 y_rows[c] = yr
-                view[c] = yr[:].rearrange("p c (j r) -> p c j r", r=2)
+                view[c] = yr[:]
                 part = slice(kc * rows, (kc + 1) * rows)
-                where[c] = q_twice[U][:, part, :].unsqueeze(2).to_broadcast([P, rows, JQ // 2, 2])
-                what[c] = v_twice[U][:, part, :].unsqueeze(2).to_broadcast([P, rows, JQ // 2, 2])
+                where[c] = q_twice[U][:, part, :].unsqueeze(2).to_broadcast([P, rows, JQ, 2])
+                what[c] = v_twice[U][:, part, :].unsqueeze(2).to_broadcast([P, rows, JQ, 2])
             for c in chunks:
                 nc.vector.tensor_tensor(
                     out=view[c],
                     in0=where[c],
-                    in1=count[:].rearrange("p (j r) -> p j r", r=2).unsqueeze(1).to_broadcast([P, rows, JQ // 2, 2]),
+                    in1=count[:].unsqueeze(1).to_broadcast([P, rows, JQ, 2]),
                     op=ALU.is_equal,
                 )
             for c in chunks:
@@ -364,20 +363,20 @@ def tile_regular_kan_w_kernel(tc, x, w_words, w_scales, t, k, out):
             for c in chunks:
                 g0 = first_pass(c)
                 nc.vector.tensor_copy(
-                    out=y_rows[c][:].rearrange("p (g a b) j -> p g a b j", a=PACK, b=DL)[:, :, PACK - 1, :, JQ - 1],
+                    out=y_rows[c][:].rearrange("p (g u b) j e -> p g u b j e", u=2, b=DL)[:, :, 1, :, JQ - 1, 1],
                     in_=silu_sb[c // chunks_per_half][:, g0 * DL : (g0 + CHUNK) * DL].rearrange("p (g b) -> p g b", b=DL),
                 )
 
         def flip(c):
-            y_flat = y_rows[c][:].rearrange("p c j -> p (c j)")
+            y_words = y_rows[c][:].rearrange("p c j e -> p (c j e)").bitcast(F32)
             gr = two_bufs.tile([P, CHUNK, P, PACK], BF16, tag="grouped", align_bytes=64)
             for b in range(CHUNK // 2):
-                yt = psum_fe.tile([P, 2, PACK, P], BF16, tag="fe")
+                yt = psum_fe.tile([P, 2, 2, P], F32, tag="fe")
                 for gi in range(2):
-                    for tt in range(PACK):
-                        col = ((2 * b + gi) * PACK + tt) * P
-                        nc.tensor.transpose(out=yt[:, gi, tt, :], in_=y_flat[:, col : col + P], identity=ident[:])
-                nc.scalar.copy(out=gr[:, 2 * b : 2 * b + 2], in_=yt[:].rearrange("p g a m -> p g m a"))
+                    for u in range(2):
+                        col = ((2 * b + gi) * 2 + u) * P
+                        nc.tensor.transpose(out=yt[:, gi, u, :], in_=y_words[:, col : col + P], identity=ident_words[:])
+                nc.scalar.copy(out=gr[:, 2 * b : 2 * b + 2].bitcast(F32), in_=yt[:].rearrange("p g u m -> p g m u"))
             grouped[c] = gr
 
         def quantise(c):

@@ -24,8 +24,8 @@ JQ = 16
 PACK = 4
 N_TILE = 512
 N_TILES = N // N_TILE
-UNIT = 8
-DU = UNIT * DL
+UNIT_SIZES = ((8, 8), (8, 8))
+DU_MAX = 8 * DL
 CHUNK = 4
 FLOPS = 2 * BATCH * D * 64 * N
 
@@ -37,7 +37,7 @@ def tile_regular_kan_w_kernel(tc, x, w_words, w_scales, t, k, out):
         keep = ctx.enter_context(tc.tile_pool(name="keep", bufs=1))
         temp = ctx.enter_context(tc.tile_pool(name="temp", bufs=1))
         two_bufs = ctx.enter_context(tc.tile_pool(name="two_bufs", bufs=2))
-        four_bufs = ctx.enter_context(tc.tile_pool(name="four_bufs", bufs=4))
+        three_bufs = ctx.enter_context(tc.tile_pool(name="three_bufs", bufs=3))
         psum_acc = ctx.enter_context(tc.psum_pool(name="acc", bufs=1))
         psum_fe = ctx.enter_context(tc.psum_pool(name="fe", bufs=4))
         ctx.enter_context(tc.manual_schedule())
@@ -53,12 +53,6 @@ def tile_regular_kan_w_kernel(tc, x, w_words, w_scales, t, k, out):
             x_half = keep.tile([P, D], BF16, name="x_half%d" % h)
             nc.sync.dma_start(out=x_half[:], in_=x[h * P : (h + 1) * P, :])
             x_sb.append(x_half)
-        silu_sb = []
-        for h in range(HALVES):
-            silu_half = keep.tile([P, D], BF16, name="silu_half%d" % h)
-            nc.scalar.activation(out=silu_half[:], in_=x_sb[h][:], func=ACT.Silu)
-            silu_sb.append(silu_half)
-
         w_planes = keep.tile([P, PASSES // 4, N], U8, align_bytes=64)
         nc.vector.memset(w_planes[:].rearrange("p s n -> p (s n)").bitcast(I32), 0)
         for slot in range(PASSES // 4):
@@ -123,24 +117,29 @@ def tile_regular_kan_w_kernel(tc, x, w_words, w_scales, t, k, out):
             out=row[:].rearrange("p a f -> p (a f)")[:, 12:64:17], in_=later[:].to_broadcast([P, PACK])
         )
 
+        terms = keep.tile([P, 8, DU_MAX], F32)
+        nc.vector.memset(terms[:, 0:8:7, :], 0.0)
+        spread = keep.tile([P, PASSES, DL, JQ], BF16)
+        nc.vector.tensor_copy(
+            out=spread[:], in_=ident[:].rearrange("p (g a) -> p g a", a=DL).unsqueeze(3).to_broadcast([P, PASSES, DL, JQ])
+        )
+        x_turned = keep.tile([P, HALVES, P], BF16)
         wn = keep.tile([P, 12], F32)
         table = keep.tile([P, PACK, DL, 16], BF16)
         y_codes = keep.tile([P, PASSES, P], U32, align_bytes=64)
         y_planes = keep.tile([P, PASSES, P], U8, align_bytes=64)
 
-        units_per_half = PASSES // UNIT
-        x_wide, x_rep, above, got, q_twice, v_twice = {}, {}, {}, {}, {}, {}
-        dist, inv, turn = {}, {}, {}
+        units = [(h, sum(UNIT_SIZES[h][:i]), UNIT_SIZES[h][i]) for h in range(HALVES) for i in range(len(UNIT_SIZES[h]))]
+        n_units = len(units)
+        chunks_per_half = PASSES // CHUNK
+        n_chunks = HALVES * chunks_per_half
+        above, got, q_planes, q_pairs, v_pairs = {}, {}, {}, {}, {}
+        y_rows, grouped, acc, summed = {}, {}, {}, {}
 
-        def planes(ap, n):
-            return ap.unsqueeze(1).to_broadcast([P, n, DU])
-
-        def x_of(U):
-            u = U % units_per_half
-            return x_sb[U // units_per_half][:, u * DU : (u + 1) * DU]
-
-        def by_pass_and_byte(twice):
-            return twice[:].rearrange("p (g u b) e -> p g u b e", u=2, b=DL)
+        def unit_of(c):
+            h, g = c // chunks_per_half, (c % chunks_per_half) * CHUNK
+            U = [i for i in range(n_units) if units[i][0] == h and units[i][1] <= g < units[i][1] + units[i][2]][0]
+            return U, g - units[U][1]
 
         def tt(out_ap, in0, in1, op):
             return lambda: nc.vector.tensor_tensor(out=out_ap, in0=in0, in1=in1, op=op)
@@ -148,151 +147,162 @@ def tile_regular_kan_w_kernel(tc, x, w_words, w_scales, t, k, out):
         def cast(out_ap, in_ap):
             return lambda: nc.vector.tensor_copy(out=out_ap, in_=in_ap)
 
-        def take_turns(one, other):
-            merged = []
-            for i in range(max(len(one), len(other))):
-                merged.extend(one[i : i + 1])
-                merged.extend(other[i : i + 1])
-            return merged
-
         def run(chain):
             for instruction in chain:
                 instruction()
 
-        def widen(U):
-            wide = two_bufs.tile([P, DU, JQ], BF16, tag="rows")
-            x_wide[U] = wide
-            return [cast(wide[:], x_of(U).unsqueeze(2).to_broadcast([P, DU, JQ]))]
+        def by_pass_and_byte(pairs):
+            return pairs[:].rearrange("p (g u b) e -> p g u b e", u=2, b=DL)
 
-        def turn_x(U):
-            flat = x_wide[U][:].rearrange("p d j -> p (d j)")
-            rep = four_bufs.tile([P, UNIT, P], BF16, tag="x_rep")
-            xt = psum_fe.tile([P, UNIT, P], BF16, tag="fe")
-            for g in range(UNIT):
-                nc.tensor.transpose(out=xt[:, g, :], in_=flat[:, g * P : (g + 1) * P], identity=ident[:])
-            nc.scalar.copy(out=rep[:], in_=xt[:])
-            x_rep[U] = rep
+        x_rep = temp.tile([P, PASSES, HALVES, P], BF16, tag="x_rep_then_results")
+
+        def turn_x():
+            xt = psum_fe.tile([P, HALVES, P], BF16, tag="fe")
+            for h in range(HALVES):
+                nc.tensor.transpose(out=xt[:, h, :], in_=x_sb[h][:], identity=ident[:])
+            nc.vector.tensor_copy(out=x_turned[:], in_=xt[:])
+
+        def replicate(g0):
+            xr = psum_fe.tile([P, 4, HALVES * P], BF16, tag="fe")
+            for g in range(g0, g0 + 4):
+                nc.tensor.matmul(
+                    out=xr[:, g - g0, :],
+                    lhsT=spread[:, g].rearrange("p a b -> p (a b)"),
+                    rhs=x_turned[:].rearrange("p h m -> p (h m)"),
+                    start=True,
+                    stop=True,
+                )
+            nc.scalar.copy(
+                out=x_rep[:, g0 : g0 + 4].rearrange("p g h m -> p (g h m)").bitcast(F32),
+                in_=xr[:].rearrange("p g m -> p (g m)").bitcast(F32),
+            )
+
+        def pair_up(pairs, by_plane, g0, ng):
+            for u in range(2):
+                nc.scalar.copy(
+                    out=by_pass_and_byte(pairs)[:, g0 : g0 + ng, u],
+                    in_=by_plane[:, 2 * u : 2 * u + 2, g0 * DL : (g0 + ng) * DL].rearrange("p e (g b) -> p g b e", b=DL),
+                )
 
         def step_plane(ab, U, a):
             return lambda: nc.vector.tensor_scalar(
-                out=ab[:, a], in0=x_rep[U][:], scalar1=wn[:, 4 + a : 5 + a], scalar2=None, op0=ALU.is_ge
+                out=ab[:, a], in0=x_rep[:, units[U][1] : units[U][1] + units[U][2], units[U][0], :], scalar1=wn[:, 4 + a : 5 + a], scalar2=None, op0=ALU.is_ge
             )
 
         def steps(U):
-            ab = two_bufs.tile([P, PACK, UNIT, P], BF16, tag="above")
+            ab = three_bufs.tile([P, PACK, units[U][2], P], BF16, tag="above_then_rows")
             above[U] = ab
             return [step_plane(ab, U, a) for a in range(PACK)]
 
-        def sums(U):
-            gt = four_bufs.tile([P, 16, DU], F32, tag="got")
-            for a in range(UNIT // 4):
-                gp = psum_fe.tile([P, 4, P], F32, tag="fe")
-                for gi in range(4):
-                    g = 4 * a + gi
-                    for b in range(PACK):
-                        nc.tensor.matmul(
-                            out=gp[:, gi, :],
-                            lhsT=above[U][:, b, g, :],
-                            rhs=table[:, b].rearrange("p a f -> p (a f)"),
-                            start=(b == 0),
-                            stop=False,
-                        )
+        def sums(j):
+            U, a = unit_of(j)
+            gp = psum_fe.tile([P, 4, P], F32, tag="fe")
+            summed[j] = gp
+            for gi in range(4):
+                g = a + gi
+                for b in range(PACK):
                     nc.tensor.matmul(
                         out=gp[:, gi, :],
-                        lhsT=x_rep[U][:, g, :],
-                        rhs=x_table[:].rearrange("p a f -> p (a f)"),
-                        start=False,
-                        stop=True,
+                        lhsT=above[U][:, b, g, :],
+                        rhs=table[:, b].rearrange("p a f -> p (a f)"),
+                        start=(b == 0),
+                        stop=False,
                     )
-                nc.scalar.copy(
-                    out=gt[:, :, 32 * a : 32 * a + 32].rearrange("p f (g a) -> p f g a", a=DL),
-                    in_=gp[:].rearrange("p g (a f) -> p f g a", f=16),
+                nc.tensor.matmul(
+                    out=gp[:, gi, :],
+                    lhsT=x_rep[:, units[U][1] + g, units[U][0], :],
+                    rhs=x_table[:].rearrange("p a f -> p (a f)"),
+                    start=False,
+                    stop=True,
                 )
-            got[U] = gt
 
-        def places(U):
-            qt = four_bufs.tile([P, UNIT * 2 * DL, 2], BF16, tag="q_twice")
-            for b in range(PACK):
-                nc.scalar.copy(
-                    out=by_pass_and_byte(qt)[:, :, b // 2, :, b % 2],
-                    in_=got[U][:, 12 + b, :].rearrange("p (g b) -> p g b", b=DL),
-                )
-            q_twice[U] = qt
+        def take(j):
+            U, a = unit_of(j)
+            du = units[U][2] * DL
+            if a == 0:
+                gt = keep.tile([P, 12, du], F32, name="got%d" % U)
+                qp = keep.tile([P, 5, du], BF16, name="q_planes%d" % U)
+                qt = keep.tile([P, units[U][2] * 2 * DL, 2], BF16, name="q_pairs%d" % U)
+                got[U], q_planes[U], q_pairs[U] = gt, qp, qt
+            cols = slice(a * DL, (a + 4) * DL)
+            by_value = summed[j][:].rearrange("p g (a f) -> p f g a", f=16)
+            nc.scalar.copy(out=got[U][:, :, cols].rearrange("p f (g a) -> p f g a", a=DL), in_=by_value[:, 0:12])
+            nc.scalar.copy(out=q_planes[U][:, 0:4, cols].rearrange("p f (g a) -> p f g a", a=DL), in_=by_value[:, 12:16])
+            nc.scalar.activation(
+                out=q_planes[U][:, 4, cols].rearrange("p (g a) -> p g a", a=DL), in_=by_value[:, 12], func=ACT.Copy, bias=-1.0
+            )
+            pair_up(q_pairs[U], q_planes[U], a, 4)
 
-        def spans(U):
-            gt = got[U]
-            ds = two_bufs.tile([P, 6, DU], F32, tag="dist")
-            tn = two_bufs.tile([P, 4, DU], BF16, tag="turn")
-            iv = two_bufs.tile([P, 4, DU], F32, tag="inv")
-            span3 = temp.tile([P, 3, DU], F32)
-            span2 = temp.tile([P, 2, DU], F32)
-            span1 = temp.tile([P, DU], F32)
-            pair = temp.tile([P, 2, DU], F32)
-            denom = temp.tile([P, 4, DU], F32)
-            two = temp.tile([P, 2, DU], F32)
-            four = temp.tile([P, DU], F32)
-            inv_four = temp.tile([P, DU], F32)
-            inv_two = temp.tile([P, 2, DU], F32)
-            dist[U], inv[U], turn[U] = ds, iv, tn
+        def compact(U):
+            ng = units[U][2]
+            du = ng * DL
+            gt, qp = got[U], q_planes[U]
+
+            def planes(ap, n):
+                return ap.unsqueeze(1).to_broadcast([P, n, du])
+
+            ds = two_bufs.tile([P, 6, du], F32, tag="ds")
+            turn = two_bufs.tile([P, 2, 4, du], BF16, tag="turn")
+            root = temp.tile([P, 4, du], F32, tag="root")
+            inv = two_bufs.tile([P, 4, du], F32, tag="inv")
+            span3 = temp.tile([P, 3, du], F32, tag="span3")
+            span2 = temp.tile([P, 2, du], F32, tag="span2")
+            span1 = temp.tile([P, du], F32, tag="span1")
+            pair = temp.tile([P, 2, du], F32, tag="pair")
+            denom = temp.tile([P, 4, du], F32, tag="denom")
+            mono = two_bufs.tile([P, 4, du], F32, tag="mono")
+            vals = temp.tile([P, 4, du], BF16, tag="vals")
+            parts = temp.tile([P, 4, 4, du], BF16, tag="parts")
+            halfway = temp.tile([P, 2, 4, du], BF16, tag="halfway")
+            by_byte = two_bufs.tile([P, 4, du], BF16, tag="by_byte")
+            vt = two_bufs.tile([P, ng * 2 * DL, 2], BF16, tag="v_pairs")
+            v_pairs[U] = vt
+            tm = terms[:, :, 0:du]
             return [
-                tt(ds[:], gt[:, 0:6, :], gt[:, 6:12, :], ALU.add),
-                tt(tn[:, 0:3, :], gt[:, 12:15, :], gt[:, 13:16, :], ALU.subtract),
-                tt(span2[:], ds[:, 3:5, :], ds[:, 1:3, :], ALU.add),
-                tt(span1[:], ds[:, 3, :], ds[:, 2, :], ALU.add),
-                tt(span3[:], ds[:, 3:6, :], ds[:, 0:3, :], ALU.add),
-                tt(pair[:], span2[:], planes(span1[:], 2), ALU.mult),
-                lambda: nc.vector.scalar_tensor_tensor(
-                    out=tn[:, 3, :], in0=gt[:, 15, :], scalar=1.0, in1=gt[:, 12, :], op0=ALU.add, op1=ALU.subtract
-                ),
-                tt(denom[:, 0:2, :], span3[:, 0:2, :], planes(pair[:, 0, :], 2), ALU.mult),
-                tt(denom[:, 2, :], span3[:, 2, :], pair[:, 1, :], ALU.mult),
-                tt(denom[:, 3, :], span3[:, 1, :], pair[:, 1, :], ALU.mult),
-                tt(two[:], denom[:, 0:4:2, :], denom[:, 1:4:2, :], ALU.mult),
-                tt(four[:], two[:, 0, :], two[:, 1, :], ALU.mult),
-                lambda: nc.vector.reciprocal(out=inv_four[:], in_=four[:]),
-                tt(inv_two[:, 0, :], inv_four[:], two[:, 1, :], ALU.mult),
-                tt(inv_two[:, 1, :], inv_four[:], two[:, 0, :], ALU.mult),
-                tt(iv[:, 0:4:2, :], inv_two[:], denom[:, 1:4:2, :], ALU.mult),
-                tt(iv[:, 1:4:2, :], inv_two[:], denom[:, 0:4:2, :], ALU.mult),
-            ]
-
-        def values(U):
-            ds, iv, tn = dist[U], inv[U], turn[U]
-            mono = temp.tile([P, 4, DU], F32)
-            left = temp.tile([P, 3, DU], F32)
-            right = temp.tile([P, 3, DU], F32)
-            vals = temp.tile([P, 8, DU], BF16)
-            both = vals[:].rearrange("p (r a) d -> p r a d", a=4)
-            by_byte = temp.tile([P, 4, DU], BF16)
-            part1 = temp.tile([P, 4, DU], BF16)
-            part2 = temp.tile([P, 4, DU], BF16)
-            part3 = temp.tile([P, 4, DU], BF16)
-            vt = two_bufs.tile([P, UNIT * 2 * DL, 2], BF16, tag="v_twice")
-            v_twice[U] = vt
-            return [
-                tt(mono[:, 1:4:2, :], ds[:, 1:3, :], ds[:, 3:5, :], ALU.mult),
-                tt(mono[:, 0, :], ds[:, 3, :], ds[:, 3, :], ALU.mult),
-                tt(mono[:, 2, :], ds[:, 2, :], ds[:, 2, :], ALU.mult),
-                tt(mono[:], mono[:], iv[:], ALU.mult),
-                tt(mono[:, 1, :], mono[:, 1, :], mono[:, 3, :], ALU.add),
-                tt(left[:], mono[:, 0:3, :], ds[:, 0:3, :], ALU.mult),
-                tt(right[:], mono[:, 0:3, :], ds[:, 3:6, :], ALU.mult),
-                cast(both[:, :, 3, :], planes(left[:, 2, :], 2)),
-                tt(
-                    both[:, :, 1:3, :],
-                    left[:, 0:2, :].unsqueeze(1).to_broadcast([P, 2, 2, DU]),
-                    right[:, 1:3, :].unsqueeze(1).to_broadcast([P, 2, 2, DU]),
-                    ALU.add,
-                ),
-                cast(both[:, :, 0, :], planes(right[:, 0, :], 2)),
-                tt(by_byte[:], vals[:, 3:7, :], planes(tn[:, 0, :], 4), ALU.mult),
-                tt(part1[:], vals[:, 2:6, :], planes(tn[:, 1, :], 4), ALU.mult),
-                tt(part2[:], vals[:, 1:5, :], planes(tn[:, 2, :], 4), ALU.mult),
-                tt(part3[:], vals[:, 0:4, :], planes(tn[:, 3, :], 4), ALU.mult),
-                tt(by_byte[:], by_byte[:], part1[:], ALU.add),
-                tt(part2[:], part2[:], part3[:], ALU.add),
-                tt(by_byte[:], by_byte[:], part2[:], ALU.add),
-                cast(by_pass_and_byte(vt), by_byte[:].rearrange("p (u e) (g b) -> p g u b e", e=2, b=DL)),
+                [
+                    tt(ds[:], gt[:, 0:6, :], gt[:, 6:12, :], ALU.add),
+                    lambda: nc.scalar.activation(out=mono[:, 0, :], in_=ds[:, 3, :], func=ACT.Square),
+                    lambda: nc.scalar.activation(out=mono[:, 2, :], in_=ds[:, 2, :], func=ACT.Square),
+                    tt(
+                        turn[:],
+                        qp[:, 0:4, :].unsqueeze(1).to_broadcast([P, 2, 4, du]),
+                        qp[:, 1:5, :].unsqueeze(1).to_broadcast([P, 2, 4, du]),
+                        ALU.subtract,
+                    ),
+                ],
+                [
+                    tt(span2[:], ds[:, 3:5, :], ds[:, 1:3, :], ALU.add),
+                    tt(span1[:], ds[:, 3, :], ds[:, 2, :], ALU.add),
+                    tt(span3[:], ds[:, 3:6, :], ds[:, 0:3, :], ALU.add),
+                ],
+                [tt(pair[:], span2[:], planes(span1[:], 2), ALU.mult)],
+                [
+                    tt(denom[:, 0:2, :], span3[:, 0:2, :], planes(pair[:, 0, :], 2), ALU.mult),
+                    tt(denom[:, 2:4, :], span3[:, 2:0:-1, :], planes(pair[:, 1, :], 2), ALU.mult),
+                    lambda: nc.scalar.activation(out=root[:], in_=denom[:], func=ACT.Abs_reciprocal_sqrt),
+                    lambda: nc.scalar.activation(out=inv[:], in_=root[:], func=ACT.Square),
+                    tt(mono[:, 1:4:2, :], ds[:, 1:3, :], ds[:, 3:5, :], ALU.mult),
+                ],
+                [tt(mono[:], mono[:], inv[:], ALU.mult)],
+                [tt(mono[:, 1, :], mono[:, 1, :], mono[:, 3, :], ALU.add)],
+                [
+                    tt(
+                        tm[:, 1:7, :].rearrange("p (s k) d -> p s k d", k=3),
+                        mono[:, 0:3, :].unsqueeze(1).to_broadcast([P, 2, 3, du]),
+                        ds[:].rearrange("p (s k) d -> p s k d", k=3),
+                        ALU.mult,
+                    ),
+                ],
+                [tt(vals[:], tm[:, 0:4, :], tm[:, 4:8, :], ALU.add)],
+                [
+                    tt(parts[:, v], planes(vals[:, v, :], 4), turn[:].rearrange("p r a d -> p (r a) d")[:, 3 - v : 7 - v, :], ALU.mult)
+                    for v in range(4)
+                ],
+                [tt(halfway[:], parts[:, 0:4:2], parts[:, 1:4:2], ALU.add)],
+                [
+                    tt(by_byte[:], halfway[:, 0], halfway[:, 1], ALU.add),
+                    lambda: pair_up(vt, by_byte, 0, ng),
+                ],
             ]
 
         def knot_table():
@@ -331,41 +341,38 @@ def tile_regular_kan_w_kernel(tc, x, w_words, w_scales, t, k, out):
             return chain
 
         rows = CHUNK * 2 * DL
-        chunks_per_unit = UNIT // CHUNK
-        chunks_per_half = PASSES // CHUNK
-        n_units = HALVES * units_per_half
-        assert chunks_per_unit == 2
-        y_rows, grouped, acc = {}, {}, {}
 
         def first_pass(c):
             return (c % chunks_per_half) * CHUNK
 
-        def expand(first, count_of):
-            chunks = range(first, first + count_of)
-            view, where, what = {}, {}, {}
-            for c in chunks:
-                U, kc = c // chunks_per_unit, c % chunks_per_unit
-                yr = two_bufs.tile([P, rows, JQ, 2], BF16, tag="rows")
-                y_rows[c] = yr
-                view[c] = yr[:]
-                part = slice(kc * rows, (kc + 1) * rows)
-                where[c] = q_twice[U][:, part, :].unsqueeze(2).to_broadcast([P, rows, JQ, 2])
-                what[c] = v_twice[U][:, part, :].unsqueeze(2).to_broadcast([P, rows, JQ, 2])
-            for c in chunks:
-                nc.vector.tensor_tensor(
-                    out=view[c],
-                    in0=where[c],
-                    in1=count[:].unsqueeze(1).to_broadcast([P, rows, JQ, 2]),
-                    op=ALU.is_equal,
-                )
-            for c in chunks:
-                nc.vector.tensor_tensor(out=view[c], in0=view[c], in1=what[c], op=ALU.mult)
-            for c in chunks:
-                g0 = first_pass(c)
-                nc.vector.tensor_copy(
-                    out=y_rows[c][:].rearrange("p (g u b) j e -> p g u b j e", u=2, b=DL)[:, :, 1, :, JQ - 1, 1],
-                    in_=silu_sb[c // chunks_per_half][:, g0 * DL : (g0 + CHUNK) * DL].rearrange("p (g b) -> p g b", b=DL),
-                )
+        def part_of(c):
+            U, g = unit_of(c)
+            return U, slice(g * 2 * DL, g * 2 * DL + rows)
+
+        def mask(c):
+            U, part = part_of(c)
+            yr = three_bufs.tile([P, rows, JQ, 2], BF16, tag="above_then_rows")
+            y_rows[c] = yr
+            nc.vector.tensor_tensor(
+                out=yr[:],
+                in0=q_pairs[U][:, part, :].unsqueeze(2).to_broadcast([P, rows, JQ, 2]),
+                in1=count[:].unsqueeze(1).to_broadcast([P, rows, JQ, 2]),
+                op=ALU.is_equal,
+            )
+
+        def fill(c):
+            U, part = part_of(c)
+            yr, g0 = y_rows[c], first_pass(c)
+            nc.vector.tensor_tensor(
+                out=yr[:],
+                in0=yr[:],
+                in1=v_pairs[U][:, part, :].unsqueeze(2).to_broadcast([P, rows, JQ, 2]),
+                op=ALU.mult,
+            )
+            nc.scalar.copy(
+                out=yr[:].rearrange("p (g u b) j e -> p g u b j e", u=2, b=DL)[:, :, 1, :, JQ - 1, 1],
+                in_=silu_sb[c // chunks_per_half][:, g0 * DL : (g0 + CHUNK) * DL].rearrange("p (g b) -> p g b", b=DL),
+            )
 
         def flip(c):
             y_words = y_rows[c][:].rearrange("p c j e -> p (c j e)").bitcast(F32)
@@ -380,13 +387,12 @@ def tile_regular_kan_w_kernel(tc, x, w_words, w_scales, t, k, out):
             grouped[c] = gr
 
         def quantise(c):
-            for b in range(CHUNK // 2):
-                g0 = first_pass(c) + 2 * b
-                nc.vector.quantize_mx(
-                    out=y_codes[:, g0 : g0 + 2, :].rearrange("p g m -> p (g m)").bitcast(FP8X4),
-                    scales=y_planes[:, g0 : g0 + 2, :].rearrange("p g m -> p (g m)"),
-                    in_=grouped[c][:, 2 * b : 2 * b + 2].rearrange("p g m a -> p (g m a)"),
-                )
+            g0 = first_pass(c)
+            nc.vector.quantize_mx(
+                out=y_codes[:, g0 : g0 + CHUNK, :].rearrange("p g m -> p (g m)").bitcast(FP8X4),
+                scales=y_planes[:, g0 : g0 + CHUNK, :].rearrange("p g m -> p (g m)"),
+                in_=grouped[c][:].rearrange("p g m a -> p (g m a)"),
+            )
 
         def multiply(c):
             h, g0 = c // chunks_per_half, first_pass(c)
@@ -394,65 +400,102 @@ def tile_regular_kan_w_kernel(tc, x, w_words, w_scales, t, k, out):
                 for nu in range(N_TILES):
                     acc_nu = psum_acc.tile([P, N_TILE], F32, name="acc%d" % nu)
                     acc[(h, nu)] = acc_nu
-            for b in range(CHUNK // 2):
-                for nu in range(N_TILES):
-                    cols = slice(nu * N_TILE, (nu + 1) * N_TILE)
-                    for g in range(g0 + 2 * b, g0 + 2 * b + 2):
-                        nc.tensor.matmul_mx(
-                            out=acc[(h, nu)][:],
-                            lhsT=y_codes[:, g, :].bitcast(FP8X4),
-                            lhsT_scale=y_planes[:, g, :],
-                            rhs=w_codes[g][:, cols].bitcast(FP8X4),
-                            rhs_scale=w_planes[4 * (g % 4) : P, g // 4, cols],
-                            start=(g == 0),
-                            stop=(g == PASSES - 1),
-                        )
+            for nu in range(N_TILES):
+                cols = slice(nu * N_TILE, (nu + 1) * N_TILE)
+                for g in range(g0, g0 + CHUNK):
+                    nc.tensor.matmul_mx(
+                        out=acc[(h, nu)][:],
+                        lhsT=y_codes[:, g, :].bitcast(FP8X4),
+                        lhsT_scale=y_planes[:, g, :],
+                        rhs=w_codes[g][:, cols].bitcast(FP8X4),
+                        rhs_scale=w_planes[4 * (g % 4) : P, g // 4, cols],
+                        start=(g == 0),
+                        stop=(g == PASSES - 1),
+                    )
 
         def store(h):
+            result = temp.tile([P, N_TILES, N_TILE], F32, tag="x_rep_then_results")
             for nu in range(N_TILES):
-                result = two_bufs.tile([P, N_TILE], F32, tag="result")
-                nc.scalar.copy(out=result[:], in_=acc[(h, nu)][:])
-                nc.sync.dma_start(out=out[h * P : (h + 1) * P, nu * N_TILE : (nu + 1) * N_TILE], in_=result[:])
+                nc.scalar.copy(out=result[:, nu, :], in_=acc[(h, nu)][:])
+                nc.sync.dma_start(out=out[h * P : (h + 1) * P, nu * N_TILE : (nu + 1) * N_TILE], in_=result[:, nu, :])
 
+        def take_turns(one, other):
+            merged = []
+            for i in range(max(len(one), len(other))):
+                merged.extend(one[i : i + 1])
+                merged.extend(other[i : i + 1])
+            return merged
 
-        table_chain = knot_table()
-        cut = len(table_chain) // 2
-        run(take_turns(table_chain[:cut], widen(0) + widen(1)))
-        turn_x(0)
-        turn_x(1)
-        run(take_turns(table_chain[cut:], widen(2) + widen(3)))
-        turn_x(2)
-        turn_x(3)
+        def flat(groups):
+            return [instruction for group in groups for instruction in group]
+
+        def spans(U):
+            chains[U] = compact(U)
+            return flat(chains[U][:4])
+
+        def values(U):
+            return flat(chains[U][4:])
+
+        chains = {}
+        warm = keep.tile([P, 2], F32)
+        nc.scalar.activation(out=warm[:, 0:1], in_=first[:], func=ACT.Silu)
+        silu_sb = []
+        for h in range(HALVES):
+            silu_half = keep.tile([P, D], BF16, name="silu_half%d" % h)
+            nc.scalar.activation(out=silu_half[:], in_=x_sb[h][:], func=ACT.Silu)
+            silu_sb.append(silu_half)
+        nc.scalar.activation(out=warm[:, 1:2], in_=first[:], func=ACT.Abs_reciprocal_sqrt, bias=1.0)
+        turn_x()
+        run(knot_table())
+        for g0 in range(0, PASSES, 4):
+            replicate(g0)
         run(steps(0))
-        run(steps(1))
         sums(0)
         sums(1)
-        run(take_turns(spans(0), steps(2) + steps(3)))
-        places(0)
-        places(1)
+        run(steps(1))
         sums(2)
         sums(3)
-        run(take_turns(values(0), spans(1)))
-        for U in range(n_units):
-            c = U * chunks_per_unit
-            expand(c, chunks_per_unit)
-            flip(c)
-            if c > 0:
-                quantise(c - 1)
-                multiply(c - 1)
-            if c > 0 and c % chunks_per_half == 0:
-                store(c // chunks_per_half - 1)
-            flip(c + 1)
-            if U + 2 < n_units:
-                places(U + 2)
-            ahead = take_turns(
-                values(U + 1) if U + 1 < n_units else [],
-                spans(U + 2) if U + 2 < n_units else [],
-            )
-            run(ahead[: len(ahead) // 2])
-            quantise(c)
-            multiply(c)
-            run(ahead[len(ahead) // 2 :])
-        quantise(n_units * chunks_per_unit - 1)
-        multiply(n_units * chunks_per_unit - 1)
-        store(HALVES - 1)
+        take(0)
+        take(1)
+        run(steps(2))
+        sums(4)
+        sums(5)
+        run(steps(3))
+        take(2)
+        run(spans(0))
+        take(3)
+        sums(6)
+        sums(7)
+        mask(0)
+        take(4)
+        take(5)
+        run(values(0))
+        mask(1)
+        take(6)
+        fill(0)
+        take(7)
+        fill(1)
+        flip(0)
+        run(spans(1))
+        flip(1)
+        quantise(0)
+        for U in range(1, n_units + 1):
+            a = 2 * U
+            multiply(a - 2)
+            if U < n_units:
+                mask(a)
+                run(values(U))
+                mask(a + 1)
+                fill(a)
+                flip(a)
+            quantise(a - 1)
+            if U < n_units:
+                fill(a + 1)
+                if U + 1 < n_units:
+                    run(spans(U + 1))
+            multiply(a - 1)
+            if a % chunks_per_half == 0:
+                store(a // chunks_per_half - 1)
+            if U < n_units:
+                flip(a + 1)
+                quantise(a)

@@ -44,25 +44,19 @@ def tile_regular_kan_w_kernel(tc, x, w_words, w_scales, t, k, out):
 
         knots16 = keep.tile([P, 4, 16], BF16)
         nc.vector.memset(knots16[:], 0.0)
-        nc.scalar.dma_start(out=knots16[1:16, 0, 0:4], in_=t[0:60].rearrange("(q c) -> q c", c=4))
-        nc.scalar.dma_start(out=knots16[0:16, 1, 0:4], in_=t[0:64].rearrange("(q c) -> q c", c=4))
-        nc.scalar.dma_start(out=knots16[0:15, 2, 0:4], in_=t[4:64].rearrange("(q c) -> q c", c=4))
-        nc.scalar.dma_start(out=knots16[15:16, 2, 0:3], in_=t[64:67].rearrange("(o c) -> o c", o=1))
         x_sb = []
         for h in range(HALVES):
             x_half = keep.tile([P, D], BF16, name="x_half%d" % h)
             nc.sync.dma_start(out=x_half[:], in_=x[h * P : (h + 1) * P, :])
             x_sb.append(x_half)
+        nc.sync.dma_start(out=knots16[1:16, 0, 0:4], in_=t[0:60].rearrange("(q c) -> q c", c=4))
+        nc.sync.dma_start(out=knots16[0:16, 1, 0:4], in_=t[0:64].rearrange("(q c) -> q c", c=4))
+        nc.sync.dma_start(out=knots16[0:15, 2, 0:4], in_=t[4:64].rearrange("(q c) -> q c", c=4))
+        nc.sync.dma_start(out=knots16[15:16, 2, 0:3], in_=t[64:67].rearrange("(o c) -> o c", o=1))
         w_planes = keep.tile([P, PASSES // 4, N], U8, align_bytes=64)
-        nc.vector.memset(w_planes[:].rearrange("p s n -> p (s n)").bitcast(I32), 0)
-        for slot in range(PASSES // 4):
-            for quad in range(4):
-                nc.sync.dma_start(
-                    out=w_planes[32 * quad : 32 * quad + 16, slot, :].bitcast(I32),
-                    in_=w_scales[4 * slot : 4 * slot + 4, 4 * quad : 4 * quad + 4, :].bitcast(I32),
-                )
         w_codes = []
-        for g in range(PASSES):
+
+        def load_codes(g):
             w_pass = keep.tile([P, N], U32, name="w_pass%d" % g, align_bytes=64)
             nc.sync.dma_start(
                 out=w_pass[:].bitcast(I32),
@@ -76,17 +70,21 @@ def tile_regular_kan_w_kernel(tc, x, w_words, w_scales, t, k, out):
         make_identity(nc, ident_words[:])
         count_i = keep.tile([P, JQ], I32)
         nc.gpsimd.iota(count_i[:], pattern=[[1, JQ]], base=0, channel_multiplier=0)
+        nc.gpsimd.memset(w_planes[:].rearrange("p s n -> p (s n)").bitcast(F32), 0.0)
+        for g in range(2):
+            load_codes(g)
+        for slot in range(PASSES // 4):
+            for quad in range(4):
+                nc.sync.dma_start(
+                    out=w_planes[32 * quad : 32 * quad + 16, slot, :].bitcast(I32),
+                    in_=w_scales[4 * slot : 4 * slot + 4, 4 * quad : 4 * quad + 4, :].bitcast(I32),
+                )
+        for g in range(2, PASSES):
+            load_codes(g)
+
         ident_dj = ident[:].rearrange("p (a b) -> p a b", b=JQ)
         sel = keep.tile([P, DL, JQ], BF16)
         nc.vector.tensor_copy(out=sel[:], in_=ident[:, 0:JQ].unsqueeze(1).to_broadcast([P, DL, JQ]))
-        rep_ps = psum_fe.tile([P, 64], F32, tag="fe")
-        nc.tensor.matmul(
-            out=rep_ps[:],
-            lhsT=sel[:].rearrange("p a b -> p (a b)"),
-            rhs=knots16[:].rearrange("p a c -> p (a c)"),
-            start=True,
-            stop=True,
-        )
         own_d = keep.tile([P, DL], F32)
         nc.vector.tensor_reduce(out=own_d[:], in_=ident_dj, axis=AX.X, op=ALU.add)
         first = keep.tile([P, 1], F32)
@@ -119,7 +117,7 @@ def tile_regular_kan_w_kernel(tc, x, w_words, w_scales, t, k, out):
 
         terms = keep.tile([P, 8, DU_MAX], F32)
         nc.vector.memset(terms[:, 0:8:7, :], 0.0)
-        spread = keep.tile([P, PASSES, DL, JQ], BF16)
+        spread = temp.tile([P, PASSES, DL, JQ], BF16, tag="spread_then_parts")
         nc.vector.tensor_copy(
             out=spread[:], in_=ident[:].rearrange("p (g a) -> p g a", a=DL).unsqueeze(3).to_broadcast([P, PASSES, DL, JQ])
         )
@@ -135,6 +133,7 @@ def tile_regular_kan_w_kernel(tc, x, w_words, w_scales, t, k, out):
         n_chunks = HALVES * chunks_per_half
         above, got, q_planes, q_pairs, v_pairs = {}, {}, {}, {}, {}
         y_rows, grouped, acc, summed = {}, {}, {}, {}
+        dist, turns, invs, monos = {}, {}, {}, {}
 
         def unit_of(c):
             h, g = c // chunks_per_half, (c % chunks_per_half) * CHUNK
@@ -147,6 +146,9 @@ def tile_regular_kan_w_kernel(tc, x, w_words, w_scales, t, k, out):
         def cast(out_ap, in_ap):
             return lambda: nc.vector.tensor_copy(out=out_ap, in_=in_ap)
 
+        def both(*instructions):
+            return lambda: run(instructions)
+
         def run(chain):
             for instruction in chain:
                 instruction()
@@ -154,7 +156,7 @@ def tile_regular_kan_w_kernel(tc, x, w_words, w_scales, t, k, out):
         def by_pass_and_byte(pairs):
             return pairs[:].rearrange("p (g u b) e -> p g u b e", u=2, b=DL)
 
-        x_rep = temp.tile([P, PASSES, HALVES, P], BF16, tag="x_rep_then_results")
+        x_rep = temp.tile([P, HALVES, PASSES, P], BF16, tag="x_rep_then_results")
 
         def turn_x():
             xt = psum_fe.tile([P, HALVES, P], BF16, tag="fe")
@@ -162,18 +164,21 @@ def tile_regular_kan_w_kernel(tc, x, w_words, w_scales, t, k, out):
                 nc.tensor.transpose(out=xt[:, h, :], in_=x_sb[h][:], identity=ident[:])
             nc.vector.tensor_copy(out=x_turned[:], in_=xt[:])
 
-        def replicate(g0):
-            xr = psum_fe.tile([P, 4, HALVES * P], BF16, tag="fe")
-            for g in range(g0, g0 + 4):
+        blocks = [(h, g0, 8) for h in range(HALVES) for g0 in range(0, PASSES, 8)]
+
+        def replicate(U):
+            h, g0, ng = blocks[U]
+            xr = psum_fe.tile([P, ng, P], BF16, tag="fe")
+            for g in range(ng):
                 nc.tensor.matmul(
-                    out=xr[:, g - g0, :],
-                    lhsT=spread[:, g].rearrange("p a b -> p (a b)"),
-                    rhs=x_turned[:].rearrange("p h m -> p (h m)"),
+                    out=xr[:, g, :],
+                    lhsT=spread[:, g0 + g].rearrange("p a b -> p (a b)"),
+                    rhs=x_turned[:, h, :],
                     start=True,
                     stop=True,
                 )
             nc.scalar.copy(
-                out=x_rep[:, g0 : g0 + 4].rearrange("p g h m -> p (g h m)").bitcast(F32),
+                out=x_rep[:, h, g0 : g0 + ng].rearrange("p g m -> p (g m)").bitcast(F32),
                 in_=xr[:].rearrange("p g m -> p (g m)").bitcast(F32),
             )
 
@@ -186,20 +191,20 @@ def tile_regular_kan_w_kernel(tc, x, w_words, w_scales, t, k, out):
 
         def step_plane(ab, U, a):
             return lambda: nc.vector.tensor_scalar(
-                out=ab[:, a], in0=x_rep[:, units[U][1] : units[U][1] + units[U][2], units[U][0], :], scalar1=wn[:, 4 + a : 5 + a], scalar2=None, op0=ALU.is_ge
+                out=ab[:, a], in0=x_rep[:, blocks[U][0], blocks[U][1] : blocks[U][1] + blocks[U][2], :], scalar1=wn[:, 4 + a : 5 + a], scalar2=None, op0=ALU.is_ge
             )
 
         def steps(U):
-            ab = three_bufs.tile([P, PACK, units[U][2], P], BF16, tag="above_then_rows")
+            ab = three_bufs.tile([P, PACK, blocks[U][2], P], BF16, tag="above_then_rows")
             above[U] = ab
             return [step_plane(ab, U, a) for a in range(PACK)]
 
         def sums(j):
-            U, a = unit_of(j)
+            U = j // 2
             gp = psum_fe.tile([P, 4, P], F32, tag="fe")
             summed[j] = gp
             for gi in range(4):
-                g = a + gi
+                g = 4 * (j % 2) + gi
                 for b in range(PACK):
                     nc.tensor.matmul(
                         out=gp[:, gi, :],
@@ -210,7 +215,7 @@ def tile_regular_kan_w_kernel(tc, x, w_words, w_scales, t, k, out):
                     )
                 nc.tensor.matmul(
                     out=gp[:, gi, :],
-                    lhsT=x_rep[:, units[U][1] + g, units[U][0], :],
+                    lhsT=x_rep[:, blocks[U][0], blocks[U][1] + g, :],
                     rhs=x_table[:].rearrange("p a f -> p (a f)"),
                     start=False,
                     stop=True,
@@ -233,79 +238,98 @@ def tile_regular_kan_w_kernel(tc, x, w_words, w_scales, t, k, out):
             )
             pair_up(q_pairs[U], q_planes[U], a, 4)
 
-        def compact(U):
-            ng = units[U][2]
-            du = ng * DL
+        def spans(U):
+            du = units[U][2] * DL
             gt, qp = got[U], q_planes[U]
 
             def planes(ap, n):
                 return ap.unsqueeze(1).to_broadcast([P, n, du])
 
-            ds = two_bufs.tile([P, 6, du], F32, tag="ds")
-            turn = two_bufs.tile([P, 2, 4, du], BF16, tag="turn")
+            ds = temp.tile([P, 6, du], F32, tag="ds")
+            turn = temp.tile([P, 2, 4, du], BF16, tag="turn")
+            inv = temp.tile([P, 4, du], F32, tag="inv")
+            mono = temp.tile([P, 4, du], F32, tag="mono")
             root = temp.tile([P, 4, du], F32, tag="root")
-            inv = two_bufs.tile([P, 4, du], F32, tag="inv")
             span3 = temp.tile([P, 3, du], F32, tag="span3")
             span2 = temp.tile([P, 2, du], F32, tag="span2")
             span1 = temp.tile([P, du], F32, tag="span1")
             pair = temp.tile([P, 2, du], F32, tag="pair")
             denom = temp.tile([P, 4, du], F32, tag="denom")
-            mono = two_bufs.tile([P, 4, du], F32, tag="mono")
-            vals = temp.tile([P, 4, du], BF16, tag="vals")
-            parts = temp.tile([P, 4, 4, du], BF16, tag="parts")
-            halfway = temp.tile([P, 2, 4, du], BF16, tag="halfway")
-            by_byte = two_bufs.tile([P, 4, du], BF16, tag="by_byte")
-            vt = two_bufs.tile([P, ng * 2 * DL, 2], BF16, tag="v_pairs")
-            v_pairs[U] = vt
-            tm = terms[:, :, 0:du]
+            dist[U], turns[U], invs[U], monos[U] = ds, turn, inv, mono
             return [
-                [
-                    tt(ds[:], gt[:, 0:6, :], gt[:, 6:12, :], ALU.add),
+                tt(ds[:], gt[:, 0:6, :], gt[:, 6:12, :], ALU.add),
+                tt(
+                    turn[:],
+                    qp[:, 0:4, :].unsqueeze(1).to_broadcast([P, 2, 4, du]),
+                    qp[:, 1:5, :].unsqueeze(1).to_broadcast([P, 2, 4, du]),
+                    ALU.subtract,
+                ),
+                both(
+                    tt(span2[:], ds[:, 3:5, :], ds[:, 1:3, :], ALU.add),
                     lambda: nc.scalar.activation(out=mono[:, 0, :], in_=ds[:, 3, :], func=ACT.Square),
                     lambda: nc.scalar.activation(out=mono[:, 2, :], in_=ds[:, 2, :], func=ACT.Square),
-                    tt(
-                        turn[:],
-                        qp[:, 0:4, :].unsqueeze(1).to_broadcast([P, 2, 4, du]),
-                        qp[:, 1:5, :].unsqueeze(1).to_broadcast([P, 2, 4, du]),
-                        ALU.subtract,
-                    ),
-                ],
-                [
-                    tt(span2[:], ds[:, 3:5, :], ds[:, 1:3, :], ALU.add),
-                    tt(span1[:], ds[:, 3, :], ds[:, 2, :], ALU.add),
-                    tt(span3[:], ds[:, 3:6, :], ds[:, 0:3, :], ALU.add),
-                ],
-                [tt(pair[:], span2[:], planes(span1[:], 2), ALU.mult)],
-                [
-                    tt(denom[:, 0:2, :], span3[:, 0:2, :], planes(pair[:, 0, :], 2), ALU.mult),
+                ),
+                tt(span1[:], ds[:, 3, :], ds[:, 2, :], ALU.add),
+                tt(span3[:], ds[:, 3:6, :], ds[:, 0:3, :], ALU.add),
+                tt(pair[:], span2[:], planes(span1[:], 2), ALU.mult),
+                tt(mono[:, 1:4:2, :], ds[:, 1:3, :], ds[:, 3:5, :], ALU.mult),
+                tt(denom[:, 0:2, :], span3[:, 0:2, :], planes(pair[:, 0, :], 2), ALU.mult),
+                both(
                     tt(denom[:, 2:4, :], span3[:, 2:0:-1, :], planes(pair[:, 1, :], 2), ALU.mult),
                     lambda: nc.scalar.activation(out=root[:], in_=denom[:], func=ACT.Abs_reciprocal_sqrt),
                     lambda: nc.scalar.activation(out=inv[:], in_=root[:], func=ACT.Square),
-                    tt(mono[:, 1:4:2, :], ds[:, 1:3, :], ds[:, 3:5, :], ALU.mult),
-                ],
-                [tt(mono[:], mono[:], inv[:], ALU.mult)],
-                [tt(mono[:, 1, :], mono[:, 1, :], mono[:, 3, :], ALU.add)],
-                [
-                    tt(
-                        tm[:, 1:7, :].rearrange("p (s k) d -> p s k d", k=3),
-                        mono[:, 0:3, :].unsqueeze(1).to_broadcast([P, 2, 3, du]),
-                        ds[:].rearrange("p (s k) d -> p s k d", k=3),
-                        ALU.mult,
-                    ),
-                ],
-                [tt(vals[:], tm[:, 0:4, :], tm[:, 4:8, :], ALU.add)],
-                [
-                    tt(parts[:, v], planes(vals[:, v, :], 4), turn[:].rearrange("p r a d -> p (r a) d")[:, 3 - v : 7 - v, :], ALU.mult)
-                    for v in range(4)
-                ],
-                [tt(halfway[:], parts[:, 0:4:2], parts[:, 1:4:2], ALU.add)],
-                [
-                    tt(by_byte[:], halfway[:, 0], halfway[:, 1], ALU.add),
-                    lambda: pair_up(vt, by_byte, 0, ng),
-                ],
+                ),
             ]
 
+        def values(U):
+            ng = units[U][2]
+            du = ng * DL
+            ds, turn, inv, mono = dist[U], turns[U], invs[U], monos[U]
+            vals = temp.tile([P, 4, du], BF16, tag="vals")
+            parts = temp.tile([P, 4, 4, du], BF16, tag="spread_then_parts")
+            halfway = temp.tile([P, 2, 4, du], BF16, tag="halfway")
+            by_byte = temp.tile([P, 4, du], BF16, tag="by_byte")
+            vt = two_bufs.tile([P, ng * 2 * DL, 2], BF16, tag="v_pairs")
+            v_pairs[U] = vt
+            tm = terms[:, :, 0:du]
+            chain = [
+                tt(mono[:], mono[:], inv[:], ALU.mult),
+                tt(mono[:, 1, :], mono[:, 1, :], mono[:, 3, :], ALU.add),
+                tt(
+                    tm[:, 1:7, :].rearrange("p (s k) d -> p s k d", k=3),
+                    mono[:, 0:3, :].unsqueeze(1).to_broadcast([P, 2, 3, du]),
+                    ds[:].rearrange("p (s k) d -> p s k d", k=3),
+                    ALU.mult,
+                ),
+                tt(vals[:], tm[:, 0:4, :], tm[:, 4:8, :], ALU.add),
+            ]
+            for v in range(4):
+                chain.append(
+                    tt(
+                        parts[:, v],
+                        vals[:, v, :].unsqueeze(1).to_broadcast([P, 4, du]),
+                        turn[:].rearrange("p r a d -> p (r a) d")[:, 3 - v : 7 - v, :],
+                        ALU.mult,
+                    )
+                )
+            chain.append(tt(halfway[:], parts[:, 0:4:2], parts[:, 1:4:2], ALU.add))
+            chain.append(
+                both(
+                    tt(by_byte[:], halfway[:, 0], halfway[:, 1], ALU.add),
+                    lambda: pair_up(vt, by_byte, 0, ng),
+                )
+            )
+            return chain
+
         def knot_table():
+            rep_ps = psum_fe.tile([P, 64], F32, tag="fe")
+            nc.tensor.matmul(
+                out=rep_ps[:],
+                lhsT=sel[:].rearrange("p a b -> p (a b)"),
+                rhs=knots16[:].rearrange("p a c -> p (a c)"),
+                start=True,
+                stop=True,
+            )
             prev = keep.tile([P, 9], F32)
             step = keep.tile([P, 9], F32)
             halves = keep.tile([P, 2, 9], BF16)
@@ -379,30 +403,30 @@ def tile_regular_kan_w_kernel(tc, x, w_words, w_scales, t, k, out):
             gr = two_bufs.tile([P, CHUNK, P, PACK], BF16, tag="grouped", align_bytes=64)
             for b in range(CHUNK // 2):
                 yt = psum_fe.tile([P, 2, 2, P], F32, tag="fe")
-                for gi in range(2):
-                    for u in range(2):
+                for u in range(2):
+                    for gi in range(2):
                         col = ((2 * b + gi) * 2 + u) * P
                         nc.tensor.transpose(out=yt[:, gi, u, :], in_=y_words[:, col : col + P], identity=ident_words[:])
                 nc.scalar.copy(out=gr[:, 2 * b : 2 * b + 2].bitcast(F32), in_=yt[:].rearrange("p g u m -> p g m u"))
             grouped[c] = gr
 
-        def quantise(c):
-            g0 = first_pass(c)
+        def quantise(c, first=0, count_of=CHUNK):
+            g0 = first_pass(c) + first
             nc.vector.quantize_mx(
-                out=y_codes[:, g0 : g0 + CHUNK, :].rearrange("p g m -> p (g m)").bitcast(FP8X4),
-                scales=y_planes[:, g0 : g0 + CHUNK, :].rearrange("p g m -> p (g m)"),
-                in_=grouped[c][:].rearrange("p g m a -> p (g m a)"),
+                out=y_codes[:, g0 : g0 + count_of, :].rearrange("p g m -> p (g m)").bitcast(FP8X4),
+                scales=y_planes[:, g0 : g0 + count_of, :].rearrange("p g m -> p (g m)"),
+                in_=grouped[c][:, first : first + count_of].rearrange("p g m a -> p (g m a)"),
             )
 
-        def multiply(c):
-            h, g0 = c // chunks_per_half, first_pass(c)
+        def multiply(c, first=0, count_of=CHUNK):
+            h, g0 = c // chunks_per_half, first_pass(c) + first
             if g0 == 0:
                 for nu in range(N_TILES):
                     acc_nu = psum_acc.tile([P, N_TILE], F32, name="acc%d" % nu)
                     acc[(h, nu)] = acc_nu
             for nu in range(N_TILES):
                 cols = slice(nu * N_TILE, (nu + 1) * N_TILE)
-                for g in range(g0, g0 + CHUNK):
+                for g in range(g0, g0 + count_of):
                     nc.tensor.matmul_mx(
                         out=acc[(h, nu)][:],
                         lhsT=y_codes[:, g, :].bitcast(FP8X4),
@@ -426,17 +450,6 @@ def tile_regular_kan_w_kernel(tc, x, w_words, w_scales, t, k, out):
                 merged.extend(other[i : i + 1])
             return merged
 
-        def flat(groups):
-            return [instruction for group in groups for instruction in group]
-
-        def spans(U):
-            chains[U] = compact(U)
-            return flat(chains[U][:4])
-
-        def values(U):
-            return flat(chains[U][4:])
-
-        chains = {}
         warm = keep.tile([P, 2], F32)
         nc.scalar.activation(out=warm[:, 0:1], in_=first[:], func=ACT.Silu)
         silu_sb = []
@@ -445,10 +458,28 @@ def tile_regular_kan_w_kernel(tc, x, w_words, w_scales, t, k, out):
             nc.scalar.activation(out=silu_half[:], in_=x_sb[h][:], func=ACT.Silu)
             silu_sb.append(silu_half)
         nc.scalar.activation(out=warm[:, 1:2], in_=first[:], func=ACT.Abs_reciprocal_sqrt, bias=1.0)
+        first_of = dict((4 * units[U][0] + units[U][1] // CHUNK, U) for U in range(n_units))
+        last_of = dict((4 * units[U][0] + (units[U][1] + units[U][2]) // CHUNK - 1, U) for U in range(n_units))
+        masked = set()
+
+        def need_mask(c):
+            if c < n_chunks and c not in masked:
+                mask(c)
+                masked.add(c)
+
+        def prepare(c):
+            need_mask(c)
+            if c in first_of:
+                run(values(first_of[c]))
+                need_mask(c + 1)
+            fill(c)
+            if c in last_of and last_of[c] + 1 < n_units:
+                run(spans(last_of[c] + 1))
+
         turn_x()
         run(knot_table())
-        for g0 in range(0, PASSES, 4):
-            replicate(g0)
+        for U in range(len(blocks)):
+            replicate(U)
         run(steps(0))
         sums(0)
         sums(1)
@@ -466,11 +497,11 @@ def tile_regular_kan_w_kernel(tc, x, w_words, w_scales, t, k, out):
         take(3)
         sums(6)
         sums(7)
-        mask(0)
+        need_mask(0)
         take(4)
         take(5)
         run(values(0))
-        mask(1)
+        need_mask(1)
         take(6)
         fill(0)
         take(7)
@@ -479,23 +510,13 @@ def tile_regular_kan_w_kernel(tc, x, w_words, w_scales, t, k, out):
         run(spans(1))
         flip(1)
         quantise(0)
-        for U in range(1, n_units + 1):
-            a = 2 * U
-            multiply(a - 2)
-            if U < n_units:
-                mask(a)
-                run(values(U))
-                mask(a + 1)
-                fill(a)
-                flip(a)
-            quantise(a - 1)
-            if U < n_units:
-                fill(a + 1)
-                if U + 1 < n_units:
-                    run(spans(U + 1))
-            multiply(a - 1)
-            if a % chunks_per_half == 0:
-                store(a // chunks_per_half - 1)
-            if U < n_units:
-                flip(a + 1)
-                quantise(a)
+        for c in range(2, n_chunks + 2):
+            if c < n_chunks:
+                prepare(c)
+            multiply(c - 2)
+            if (c - 1) % chunks_per_half == 0:
+                store((c - 2) // chunks_per_half)
+            if c < n_chunks:
+                flip(c)
+            if c - 1 < n_chunks:
+                quantise(c - 1)

@@ -70,16 +70,21 @@ def tile_regular_kan_w_kernel(tc, x, w_words, w_scales, t, k, out):
         make_identity(nc, ident_words[:])
         count_i = keep.tile([P, JQ], I32)
         nc.gpsimd.iota(count_i[:], pattern=[[1, JQ]], base=0, channel_multiplier=0)
-        nc.gpsimd.memset(w_planes[:].rearrange("p s n -> p (s n)").bitcast(F32), 0.0)
-        for g in range(2):
-            load_codes(g)
         for slot in range(PASSES // 4):
             for quad in range(4):
-                nc.sync.dma_start(
-                    out=w_planes[32 * quad : 32 * quad + 16, slot, :].bitcast(I32),
-                    in_=w_scales[4 * slot : 4 * slot + 4, 4 * quad : 4 * quad + 4, :].bitcast(I32),
-                )
-        for g in range(2, PASSES):
+                rows_of = slice(4 * quad, 4 * quad + 4)
+                if 4 * slot + 8 <= PASSES:
+                    nc.sync.dma_start(
+                        out=w_planes[32 * quad : 32 * quad + 32, slot, :].bitcast(I32),
+                        in_=w_scales[4 * slot : 4 * slot + 8, rows_of, :].bitcast(I32),
+                    )
+                else:
+                    for part in range(2):
+                        nc.sync.dma_start(
+                            out=w_planes[32 * quad + 16 * part : 32 * quad + 16 * part + 16, slot, :].bitcast(I32),
+                            in_=w_scales[4 * slot - 4 * part : 4 * slot - 4 * part + 4, rows_of, :].bitcast(I32),
+                        )
+        for g in range(PASSES):
             load_codes(g)
 
         ident_dj = ident[:].rearrange("p (a b) -> p a b", b=JQ)

@@ -87,24 +87,39 @@ def tile_regular_kan_w_kernel(tc, x, w_words, w_scales, t, k, out):
         for g in range(PASSES):
             load_codes(g)
 
-        ident_dj = ident[:].rearrange("p (a b) -> p a b", b=JQ)
-        sel = keep.tile([P, DL, JQ], BF16)
-        nc.vector.tensor_copy(out=sel[:], in_=ident[:, 0:JQ].unsqueeze(1).to_broadcast([P, DL, JQ]))
-        own_d = keep.tile([P, DL], F32)
-        nc.vector.tensor_reduce(out=own_d[:], in_=ident_dj, axis=AX.X, op=ALU.add)
-        first = keep.tile([P, 1], F32)
-        nc.vector.tensor_reduce(out=first[:], in_=ident_dj[:, :, 0], axis=AX.X, op=ALU.add)
-        later = keep.tile([P, 1], F32)
-        nc.vector.tensor_scalar(out=later[:], in0=first[:], scalar1=-1.0, scalar2=1.0, op0=ALU.mult, op1=ALU.add)
         sign = keep.tile([P, PACK, 6], F32)
         nc.vector.memset(sign[:, :, 0:3], -1.0)
         nc.vector.memset(sign[:, :, 3:6], 1.0)
-        nc.vector.tensor_scalar(out=sign[:, 0:3, :], in0=sign[:, 0:3, :], scalar1=later[:], scalar2=None, op0=ALU.mult)
         x_row = keep.tile([P, 16], F32)
         nc.vector.memset(x_row[:], 0.0)
         nc.vector.memset(x_row[:, 0:3], 1.0)
         nc.vector.memset(x_row[:, 3:6], -1.0)
+        row = keep.tile([P, PACK, 16], BF16)
+        nc.vector.memset(row[:], 0.0)
+        terms = keep.tile([P, 8, DU_MAX], F32)
+        nc.vector.memset(terms[:, 0:8:7, :], 0.0)
+        ident_dj = ident[:].rearrange("p (a b) -> p a b", b=JQ)
+        sel = keep.tile([P, DL, JQ], BF16)
+        nc.vector.tensor_copy(out=sel[:], in_=ident[:, 0:JQ].unsqueeze(1).to_broadcast([P, DL, JQ]))
+        spread = temp.tile([P, PASSES, DL, JQ], BF16, tag="spread_then_parts")
+        nc.vector.tensor_copy(
+            out=spread[:], in_=ident[:].rearrange("p (g a) -> p g a", a=DL).unsqueeze(3).to_broadcast([P, PASSES, DL, JQ])
+        )
+        own_d = keep.tile([P, DL], F32)
+        nc.vector.tensor_reduce(out=own_d[:], in_=ident_dj, axis=AX.X, op=ALU.add)
+        first = keep.tile([P, 1], F32)
+        nc.vector.tensor_reduce(out=first[:], in_=ident_dj[:, :, 0], axis=AX.X, op=ALU.add)
+        count = keep.tile([P, JQ, 2], BF16)
+        nc.vector.tensor_copy(out=count[:], in_=count_i[:].unsqueeze(2).to_broadcast([P, JQ, 2]))
+        later = keep.tile([P, 1], F32)
+        nc.vector.tensor_scalar(out=later[:], in0=first[:], scalar1=-1.0, scalar2=1.0, op0=ALU.mult, op1=ALU.add)
         nc.vector.tensor_scalar(out=x_row[:], in0=x_row[:], scalar1=first[:], scalar2=None, op0=ALU.mult)
+        minus_later = keep.tile([P, 1], F32)
+        nc.vector.tensor_scalar(out=minus_later[:], in0=first[:], scalar1=-1.0, scalar2=None, op0=ALU.add)
+        nc.vector.tensor_scalar(out=sign[:, 0:3, :], in0=sign[:, 0:3, :], scalar1=later[:], scalar2=None, op0=ALU.mult)
+        nc.vector.tensor_copy(
+            out=row[:].rearrange("p a f -> p (a f)")[:, 12:64:17], in_=later[:].to_broadcast([P, PACK])
+        )
         x_table = keep.tile([P, DL, 16], BF16)
         nc.vector.tensor_tensor(
             out=x_table[:],
@@ -112,20 +127,7 @@ def tile_regular_kan_w_kernel(tc, x, w_words, w_scales, t, k, out):
             in1=own_d[:].unsqueeze(2).to_broadcast([P, DL, 16]),
             op=ALU.mult,
         )
-        count = keep.tile([P, JQ, 2], BF16)
-        nc.vector.tensor_copy(out=count[:], in_=count_i[:].unsqueeze(2).to_broadcast([P, JQ, 2]))
-        row = keep.tile([P, PACK, 16], BF16)
-        nc.vector.memset(row[:], 0.0)
-        nc.vector.tensor_copy(
-            out=row[:].rearrange("p a f -> p (a f)")[:, 12:64:17], in_=later[:].to_broadcast([P, PACK])
-        )
 
-        terms = keep.tile([P, 8, DU_MAX], F32)
-        nc.vector.memset(terms[:, 0:8:7, :], 0.0)
-        spread = temp.tile([P, PASSES, DL, JQ], BF16, tag="spread_then_parts")
-        nc.vector.tensor_copy(
-            out=spread[:], in_=ident[:].rearrange("p (g a) -> p g a", a=DL).unsqueeze(3).to_broadcast([P, PASSES, DL, JQ])
-        )
         x_turned = keep.tile([P, HALVES, P], BF16)
         wn = keep.tile([P, 12], F32)
         table = keep.tile([P, PACK, DL, 16], BF16)
@@ -171,7 +173,7 @@ def tile_regular_kan_w_kernel(tc, x, w_words, w_scales, t, k, out):
 
         blocks = [(h, g0, 8) for h in range(HALVES) for g0 in range(0, PASSES, 8)]
 
-        def replicate(U):
+        def replicate(U, engine):
             h, g0, ng = blocks[U]
             xr = psum_fe.tile([P, ng, P], BF16, tag="fe")
             for g in range(ng):
@@ -182,7 +184,7 @@ def tile_regular_kan_w_kernel(tc, x, w_words, w_scales, t, k, out):
                     start=True,
                     stop=True,
                 )
-            nc.scalar.copy(
+            engine(
                 out=x_rep[:, h, g0 : g0 + ng].rearrange("p g m -> p (g m)").bitcast(F32),
                 in_=xr[:].rearrange("p g m -> p (g m)").bitcast(F32),
             )
@@ -194,15 +196,21 @@ def tile_regular_kan_w_kernel(tc, x, w_words, w_scales, t, k, out):
                     in_=by_plane[:, 2 * u : 2 * u + 2, g0 * DL : (g0 + ng) * DL].rearrange("p e (g b) -> p g b e", b=DL),
                 )
 
-        def step_plane(ab, U, a):
+        def step_plane(ab, U, a, first, count_of):
+            g0 = blocks[U][1] + first
             return lambda: nc.vector.tensor_scalar(
-                out=ab[:, a], in0=x_rep[:, blocks[U][0], blocks[U][1] : blocks[U][1] + blocks[U][2], :], scalar1=wn[:, 4 + a : 5 + a], scalar2=None, op0=ALU.is_ge
+                out=ab[:, a, first : first + count_of],
+                in0=x_rep[:, blocks[U][0], g0 : g0 + count_of, :],
+                scalar1=wn[:, 4 + a : 5 + a],
+                scalar2=None,
+                op0=ALU.is_ge,
             )
 
-        def steps(U):
+        def steps(U, parts=1):
             ab = three_bufs.tile([P, PACK, blocks[U][2], P], BF16, tag="above_then_rows")
             above[U] = ab
-            return [step_plane(ab, U, a) for a in range(PACK)]
+            width = blocks[U][2] // parts
+            return [step_plane(ab, U, a, part * width, width) for part in range(parts) for a in range(PACK)]
 
         def sums(j):
             U = j // 2
@@ -335,7 +343,6 @@ def tile_regular_kan_w_kernel(tc, x, w_words, w_scales, t, k, out):
                 start=True,
                 stop=True,
             )
-            prev = keep.tile([P, 9], F32)
             step = keep.tile([P, 9], F32)
             halves = keep.tile([P, 2, 9], BF16)
             chain = [
@@ -343,10 +350,9 @@ def tile_regular_kan_w_kernel(tc, x, w_words, w_scales, t, k, out):
                     wn[:].rearrange("p (a c) -> p a c", c=4),
                     rep_ps[:].rearrange("p (a c) -> p a c", c=16)[:, 0:3, 0:4],
                 ),
-                lambda: nc.vector.tensor_scalar(
-                    out=prev[:], in0=wn[:, 1:10], scalar1=later[:], scalar2=None, op0=ALU.mult
+                lambda: nc.vector.scalar_tensor_tensor(
+                    out=step[:], in0=wn[:, 1:10], scalar=minus_later[:], in1=wn[:, 2:11], op0=ALU.mult, op1=ALU.add
                 ),
-                tt(step[:], wn[:, 2:11], prev[:], ALU.subtract),
                 cast(halves[:, 0, :], step[:]),
                 tt(halves[:, 1, :], step[:], halves[:, 0, :], ALU.subtract),
             ]
@@ -483,9 +489,10 @@ def tile_regular_kan_w_kernel(tc, x, w_words, w_scales, t, k, out):
 
         turn_x()
         run(knot_table())
-        for U in range(len(blocks)):
-            replicate(U)
-        run(steps(0))
+        replicate(0, nc.scalar.copy)
+        for U in range(1, len(blocks)):
+            replicate(U, nc.scalar.copy)
+        run(steps(0, 2))
         sums(0)
         sums(1)
         run(steps(1))

@@ -42,17 +42,13 @@ def tile_regular_kan_w_kernel(tc, x, w_words, w_scales, t, k, out):
         psum_fe = ctx.enter_context(tc.psum_pool(name="fe", bufs=4))
         ctx.enter_context(tc.manual_schedule())
 
-        knots16 = keep.tile([P, 4, 16], BF16)
-        nc.vector.memset(knots16[:], 0.0)
-        x_sb = []
-        for h in range(HALVES):
-            x_half = keep.tile([P, D], BF16, name="x_half%d" % h)
-            nc.sync.dma_start(out=x_half[:], in_=x[h * P : (h + 1) * P, :])
-            x_sb.append(x_half)
-        nc.sync.dma_start(out=knots16[1:16, 0, 0:4], in_=t[0:60].rearrange("(q c) -> q c", c=4))
-        nc.sync.dma_start(out=knots16[0:16, 1, 0:4], in_=t[0:64].rearrange("(q c) -> q c", c=4))
-        nc.sync.dma_start(out=knots16[0:15, 2, 0:4], in_=t[4:64].rearrange("(q c) -> q c", c=4))
-        nc.sync.dma_start(out=knots16[15:16, 2, 0:3], in_=t[64:67].rearrange("(o c) -> o c", o=1))
+        x_all = keep.tile([P, HALVES, D], BF16)
+        nc.sync.dma_start(out=x_all[:], in_=x.rearrange("(h p) d -> p h d", p=P))
+        x_sb = [x_all[:, h, :] for h in range(HALVES)]
+        knot_rows = keep.tile([P, 4], BF16)
+        nc.vector.memset(knot_rows[:], 0.0)
+        nc.sync.dma_start(out=knot_rows[1:17, :], in_=t[0:64].rearrange("(q c) -> q c", c=4))
+        nc.sync.dma_start(out=knot_rows[17:18, 0:3], in_=t[64:67].rearrange("(o c) -> o c", o=1))
         w_planes = keep.tile([P, PASSES // 4, N], U8, align_bytes=64)
         w_codes = []
 
@@ -70,6 +66,8 @@ def tile_regular_kan_w_kernel(tc, x, w_words, w_scales, t, k, out):
         make_identity(nc, ident_words[:])
         count_i = keep.tile([P, JQ], I32)
         nc.gpsimd.iota(count_i[:], pattern=[[1, JQ]], base=0, channel_multiplier=0)
+        for g in range(4):
+            load_codes(g)
         for slot in range(PASSES // 4):
             for quad in range(4):
                 rows_of = slice(4 * quad, 4 * quad + 4)
@@ -84,7 +82,7 @@ def tile_regular_kan_w_kernel(tc, x, w_words, w_scales, t, k, out):
                             out=w_planes[32 * quad + 16 * part : 32 * quad + 16 * part + 16, slot, :].bitcast(I32),
                             in_=w_scales[4 * slot - 4 * part : 4 * slot - 4 * part + 4, rows_of, :].bitcast(I32),
                         )
-        for g in range(PASSES):
+        for g in range(4, PASSES):
             load_codes(g)
 
         sign = keep.tile([P, PACK, 6], F32)
@@ -99,8 +97,9 @@ def tile_regular_kan_w_kernel(tc, x, w_words, w_scales, t, k, out):
         terms = keep.tile([P, 8, DU_MAX], F32)
         nc.vector.memset(terms[:, 0:8:7, :], 0.0)
         ident_dj = ident[:].rearrange("p (a b) -> p a b", b=JQ)
-        sel = keep.tile([P, DL, JQ], BF16)
-        nc.vector.tensor_copy(out=sel[:], in_=ident[:, 0:JQ].unsqueeze(1).to_broadcast([P, DL, JQ]))
+        sel = keep.tile([P, 3, DL, JQ], BF16)
+        for a in range(3):
+            nc.vector.tensor_copy(out=sel[:, a], in_=ident[:, a : a + JQ].unsqueeze(1).to_broadcast([P, DL, JQ]))
         spread = temp.tile([P, PASSES, DL, JQ], BF16, tag="spread_then_parts")
         nc.vector.tensor_copy(
             out=spread[:], in_=ident[:].rearrange("p (g a) -> p g a", a=DL).unsqueeze(3).to_broadcast([P, PASSES, DL, JQ])
@@ -168,7 +167,7 @@ def tile_regular_kan_w_kernel(tc, x, w_words, w_scales, t, k, out):
         def turn_x():
             xt = psum_fe.tile([P, HALVES, P], BF16, tag="fe")
             for h in range(HALVES):
-                nc.tensor.transpose(out=xt[:, h, :], in_=x_sb[h][:], identity=ident[:])
+                nc.tensor.transpose(out=xt[:, h, :], in_=x_sb[h], identity=ident[:])
             nc.vector.tensor_copy(out=x_turned[:], in_=xt[:])
 
         blocks = [(h, g0, 8) for h in range(HALVES) for g0 in range(0, PASSES, 8)]
@@ -258,10 +257,10 @@ def tile_regular_kan_w_kernel(tc, x, w_words, w_scales, t, k, out):
             def planes(ap, n):
                 return ap.unsqueeze(1).to_broadcast([P, n, du])
 
-            ds = temp.tile([P, 6, du], F32, tag="ds")
-            turn = temp.tile([P, 2, 4, du], BF16, tag="turn")
-            inv = temp.tile([P, 4, du], F32, tag="inv")
-            mono = temp.tile([P, 4, du], F32, tag="mono")
+            ds = two_bufs.tile([P, 6, du], F32, tag="ds")
+            turn = two_bufs.tile([P, 2, 4, du], BF16, tag="turn")
+            inv = two_bufs.tile([P, 4, du], F32, tag="inv")
+            mono = two_bufs.tile([P, 4, du], F32, tag="mono")
             root = temp.tile([P, 4, du], F32, tag="root")
             span3 = temp.tile([P, 3, du], F32, tag="span3")
             span2 = temp.tile([P, 2, du], F32, tag="span2")
@@ -335,20 +334,21 @@ def tile_regular_kan_w_kernel(tc, x, w_words, w_scales, t, k, out):
             return chain
 
         def knot_table():
-            rep_ps = psum_fe.tile([P, 64], F32, tag="fe")
-            nc.tensor.matmul(
-                out=rep_ps[:],
-                lhsT=sel[:].rearrange("p a b -> p (a b)"),
-                rhs=knots16[:].rearrange("p a c -> p (a c)"),
-                start=True,
-                stop=True,
-            )
+            rep_ps = psum_fe.tile([P, 3, 4], F32, tag="fe")
+            for a in range(3):
+                nc.tensor.matmul(
+                    out=rep_ps[:, a, :],
+                    lhsT=sel[:, a].rearrange("p a b -> p (a b)"),
+                    rhs=knot_rows[:],
+                    start=True,
+                    stop=True,
+                )
             step = keep.tile([P, 9], F32)
             halves = keep.tile([P, 2, 9], BF16)
             chain = [
                 cast(
                     wn[:].rearrange("p (a c) -> p a c", c=4),
-                    rep_ps[:].rearrange("p (a c) -> p a c", c=16)[:, 0:3, 0:4],
+                    rep_ps[:],
                 ),
                 lambda: nc.vector.scalar_tensor_tensor(
                     out=step[:], in0=wn[:, 1:10], scalar=minus_later[:], in1=wn[:, 2:11], op0=ALU.mult, op1=ALU.add
@@ -466,7 +466,7 @@ def tile_regular_kan_w_kernel(tc, x, w_words, w_scales, t, k, out):
         silu_sb = []
         for h in range(HALVES):
             silu_half = keep.tile([P, D], BF16, name="silu_half%d" % h)
-            nc.scalar.activation(out=silu_half[:], in_=x_sb[h][:], func=ACT.Silu)
+            nc.scalar.activation(out=silu_half[:], in_=x_sb[h], func=ACT.Silu)
             silu_sb.append(silu_half)
         nc.scalar.activation(out=warm[:, 1:2], in_=first[:], func=ACT.Abs_reciprocal_sqrt, bias=1.0)
         first_of = dict((4 * units[U][0] + units[U][1] // CHUNK, U) for U in range(n_units))
@@ -478,18 +478,36 @@ def tile_regular_kan_w_kernel(tc, x, w_words, w_scales, t, k, out):
                 mask(c)
                 masked.add(c)
 
+        left = {}
+
+        def lace(chain, other):
+            laced, at = [], 0
+            for i in range(len(chain)):
+                laced.append(chain[i])
+                if i in (0, 1, 2, 3, 7, 8) and at < len(other):
+                    laced.append(other[at])
+                    at += 1
+            return laced, other[at:]
+
         def prepare(c):
             need_mask(c)
             if c in first_of:
-                run(values(first_of[c]))
+                U = first_of[c]
+                if U >= 1 and U + 1 < n_units:
+                    laced, left[U + 1] = lace(values(U), spans(U + 1))
+                    run(laced)
+                else:
+                    run(values(U))
                 need_mask(c + 1)
             fill(c)
             if c in last_of and last_of[c] + 1 < n_units:
-                run(spans(last_of[c] + 1))
+                run(left[last_of[c] + 1] if last_of[c] + 1 in left else spans(last_of[c] + 1))
 
         turn_x()
-        run(knot_table())
-        replicate(0, nc.scalar.copy)
+        table_chain = knot_table()
+        run(table_chain[:4])
+        replicate(0, nc.vector.tensor_copy)
+        run(table_chain[4:])
         for U in range(1, len(blocks)):
             replicate(U, nc.scalar.copy)
         run(steps(0, 2))
@@ -512,15 +530,17 @@ def tile_regular_kan_w_kernel(tc, x, w_words, w_scales, t, k, out):
         need_mask(0)
         take(4)
         take(5)
-        run(values(0))
+        laced, left[1] = lace(values(0), spans(1))
+        run(laced)
         need_mask(1)
         take(6)
         fill(0)
         take(7)
         fill(1)
         flip(0)
-        run(spans(1))
+        run(left[1])
         flip(1)
+        need_mask(2)
         quantise(0)
         for c in range(2, n_chunks + 2):
             if c < n_chunks:

@@ -435,18 +435,22 @@ def tile_regular_kan_w_kernel(tc, x, w_words, w_scales, t, k, out):
                 for nu in range(N_TILES):
                     acc_nu = psum_acc.tile([P, N_TILE], F32, name="acc%d" % nu)
                     acc[(h, nu)] = acc_nu
-            for nu in range(N_TILES):
+            passes = range(g0, g0 + count_of)
+            if h == 0:
+                order = [(g, nu) for g in passes for nu in range(N_TILES)]
+            else:
+                order = [(g, nu) for nu in range(N_TILES) for g in passes]
+            for g, nu in order:
                 cols = slice(nu * N_TILE, (nu + 1) * N_TILE)
-                for g in range(g0, g0 + count_of):
-                    nc.tensor.matmul_mx(
-                        out=acc[(h, nu)][:],
-                        lhsT=y_codes[:, g, :].bitcast(FP8X4),
-                        lhsT_scale=y_planes[:, g, :],
-                        rhs=w_codes[g][:, cols].bitcast(FP8X4),
-                        rhs_scale=w_planes[4 * (g % 4) : P, g // 4, cols],
-                        start=(g == 0),
-                        stop=(g == PASSES - 1),
-                    )
+                nc.tensor.matmul_mx(
+                    out=acc[(h, nu)][:],
+                    lhsT=y_codes[:, g, :].bitcast(FP8X4),
+                    lhsT_scale=y_planes[:, g, :],
+                    rhs=w_codes[g][:, cols].bitcast(FP8X4),
+                    rhs_scale=w_planes[4 * (g % 4) : P, g // 4, cols],
+                    start=(g == 0),
+                    stop=(g == PASSES - 1),
+                )
 
         def store(h):
             result = temp.tile([P, N_TILES, N_TILE], F32, tag="x_rep_then_results")

from contextlib import ExitStack

import concourse.mybir as mybir
from concourse.masks import make_identity

F32 = mybir.dt.float32
BF16 = mybir.dt.bfloat16
I32 = mybir.dt.int32
U32 = mybir.dt.uint32
U8 = mybir.dt.uint8
FP8X4 = mybir.dt.float8_e4m3fn_x4
ALU = mybir.AluOpType
ACT = mybir.ActivationFunctionType
AX = mybir.AxisListType

P = 128
BATCH = 256
HALVES = BATCH // P
D = 128
N = 2048
PASSES = 16
DL = 8
JQ = 16
PACK = 4
N_TILE = 512
N_TILES = N // N_TILE
UNIT_SIZES = ((8, 8), (8, 8))
DU_MAX = 8 * DL
CHUNK = 4
FLOPS = 2 * BATCH * D * 64 * N


def tile_regular_kan_w_kernel(tc, x, w_words, w_scales, t, k, out):
    nc = tc.nc
    assert k == 4
    with ExitStack() as ctx:
        keep = ctx.enter_context(tc.tile_pool(name="keep", bufs=1))
        temp = ctx.enter_context(tc.tile_pool(name="temp", bufs=1))
        two_bufs = ctx.enter_context(tc.tile_pool(name="two_bufs", bufs=2))
        three_bufs = ctx.enter_context(tc.tile_pool(name="three_bufs", bufs=3))
        psum_acc = ctx.enter_context(tc.psum_pool(name="acc", bufs=1))
        psum_fe = ctx.enter_context(tc.psum_pool(name="fe", bufs=4))
        ctx.enter_context(tc.manual_schedule())

        x_all = keep.tile([P, HALVES, D], BF16)
        nc.sync.dma_start(out=x_all[:], in_=x.rearrange("(h p) d -> p h d", p=P))
        x_sb = [x_all[:, h, :] for h in range(HALVES)]
        knot_rows = keep.tile([P, 4], BF16)
        nc.vector.memset(knot_rows[:], 0.0)
        nc.sync.dma_start(out=knot_rows[1:17, :], in_=t[0:64].rearrange("(q c) -> q c", c=4))
        nc.sync.dma_start(out=knot_rows[17:18, 0:3], in_=t[64:67].rearrange("(o c) -> o c", o=1))
        w_planes = keep.tile([P, PASSES // 4, N], U8, align_bytes=64)
        w_codes = []

        def load_codes(g):
            w_pass = keep.tile([P, N], U32, name="w_pass%d" % g, align_bytes=64)
            nc.sync.dma_start(
                out=w_pass[:].bitcast(I32),
                in_=w_words[g].rearrange("p n c -> p (n c)").bitcast(I32),
            )
            w_codes.append(w_pass)

        ident = keep.tile([P, P], BF16)
        make_identity(nc, ident[:])
        ident_words = keep.tile([P, P], F32)
        make_identity(nc, ident_words[:])
        count_i = keep.tile([P, JQ], I32)
        nc.gpsimd.iota(count_i[:], pattern=[[1, JQ]], base=0, channel_multiplier=0)
        for g in range(4):
            load_codes(g)
        for slot in range(PASSES // 4):
            for quad in range(4):
                rows_of = slice(4 * quad, 4 * quad + 4)
                if 4 * slot + 8 <= PASSES:
                    nc.sync.dma_start(
                        out=w_planes[32 * quad : 32 * quad + 32, slot, :].bitcast(I32),
                        in_=w_scales[4 * slot : 4 * slot + 8, rows_of, :].bitcast(I32),
                    )
                else:
                    for part in range(2):
                        nc.sync.dma_start(
                            out=w_planes[32 * quad + 16 * part : 32 * quad + 16 * part + 16, slot, :].bitcast(I32),
                            in_=w_scales[4 * slot - 4 * part : 4 * slot - 4 * part + 4, rows_of, :].bitcast(I32),
                        )
        for g in range(4, PASSES):
            load_codes(g)

        sign = keep.tile([P, PACK, 6], F32)
        nc.vector.memset(sign[:, :, 0:3], -1.0)
        nc.vector.memset(sign[:, :, 3:6], 1.0)
        x_row = keep.tile([P, 16], F32)
        nc.vector.memset(x_row[:], 0.0)
        nc.vector.memset(x_row[:, 0:3], 1.0)
        nc.vector.memset(x_row[:, 3:6], -1.0)
        row = keep.tile([P, PACK, 16], BF16)
        nc.vector.memset(row[:], 0.0)
        terms = keep.tile([P, 8, DU_MAX], F32)
        nc.vector.memset(terms[:, 0:8:7, :], 0.0)
        ident_dj = ident[:].rearrange("p (a b) -> p a b", b=JQ)
        sel = keep.tile([P, 3, DL, JQ], BF16)
        for a in range(3):
            nc.vector.tensor_copy(out=sel[:, a], in_=ident[:, a : a + JQ].unsqueeze(1).to_broadcast([P, DL, JQ]))
        spread = temp.tile([P, PASSES, DL, JQ], BF16, tag="spread_then_parts")
        nc.vector.tensor_copy(
            out=spread[:], in_=ident[:].rearrange("p (g a) -> p g a", a=DL).unsqueeze(3).to_broadcast([P, PASSES, DL, JQ])
        )
        own_d = keep.tile([P, DL], F32)
        nc.vector.tensor_reduce(out=own_d[:], in_=ident_dj, axis=AX.X, op=ALU.add)
        first = keep.tile([P, 1], F32)
        nc.vector.tensor_reduce(out=first[:], in_=ident_dj[:, :, 0], axis=AX.X, op=ALU.add)
        count = keep.tile([P, JQ, 2], BF16)
        nc.vector.tensor_copy(out=count[:], in_=count_i[:].unsqueeze(2).to_broadcast([P, JQ, 2]))
        later = keep.tile([P, 1], F32)
        nc.vector.tensor_scalar(out=later[:], in0=first[:], scalar1=-1.0, scalar2=1.0, op0=ALU.mult, op1=ALU.add)
        nc.vector.tensor_scalar(out=x_row[:], in0=x_row[:], scalar1=first[:], scalar2=None, op0=ALU.mult)
        minus_later = keep.tile([P, 1], F32)
        nc.vector.tensor_scalar(out=minus_later[:], in0=first[:], scalar1=-1.0, scalar2=None, op0=ALU.add)
        nc.vector.tensor_scalar(out=sign[:, 0:3, :], in0=sign[:, 0:3, :], scalar1=later[:], scalar2=None, op0=ALU.mult)
        nc.vector.tensor_copy(
            out=row[:].rearrange("p a f -> p (a f)")[:, 12:64:17], in_=later[:].to_broadcast([P, PACK])
        )
        x_table = keep.tile([P, DL, 16], BF16)
        nc.vector.tensor_tensor(
            out=x_table[:],
            in0=x_row[:].unsqueeze(1).to_broadcast([P, DL, 16]),
            in1=own_d[:].unsqueeze(2).to_broadcast([P, DL, 16]),
            op=ALU.mult,
        )

        x_turned = keep.tile([P, HALVES, P], BF16)
        wn = keep.tile([P, 12], F32)
        table = keep.tile([P, PACK, DL, 16], BF16)
        y_codes = keep.tile([P, PASSES, P], U32, align_bytes=64)
        y_planes = keep.tile([P, PASSES, P], U8, align_bytes=64)

        units = [(h, sum(UNIT_SIZES[h][:i]), UNIT_SIZES[h][i]) for h in range(HALVES) for i in range(len(UNIT_SIZES[h]))]
        n_units = len(units)
        chunks_per_half = PASSES // CHUNK
        n_chunks = HALVES * chunks_per_half
        above, got, q_planes, q_pairs, v_pairs = {}, {}, {}, {}, {}
        y_rows, grouped, acc, summed = {}, {}, {}, {}
        dist, turns, invs, monos = {}, {}, {}, {}

        def unit_of(c):
            h, g = c // chunks_per_half, (c % chunks_per_half) * CHUNK
            U = [i for i in range(n_units) if units[i][0] == h and units[i][1] <= g < units[i][1] + units[i][2]][0]
            return U, g - units[U][1]

        def tt(out_ap, in0, in1, op):
            return lambda: nc.vector.tensor_tensor(out=out_ap, in0=in0, in1=in1, op=op)

        def cast(out_ap, in_ap):
            return lambda: nc.vector.tensor_copy(out=out_ap, in_=in_ap)

        def both(*instructions):
            return lambda: run(instructions)

        def run(chain):
            for instruction in chain:
                instruction()

        def by_pass_and_byte(pairs):
            return pairs[:].rearrange("p (g u b) e -> p g u b e", u=2, b=DL)

        x_rep = temp.tile([P, HALVES, PASSES, P], BF16, tag="x_rep_then_results")

        def turn_x():
            xt = psum_fe.tile([P, HALVES, P], BF16, tag="fe")
            for h in range(HALVES):
                nc.tensor.transpose(out=xt[:, h, :], in_=x_sb[h], identity=ident[:])
            nc.vector.tensor_copy(out=x_turned[:], in_=xt[:])

        blocks = [(h, g0, 8) for h in range(HALVES) for g0 in range(0, PASSES, 8)]

        def replicate(U, engine):
            h, g0, ng = blocks[U]
            xr = psum_fe.tile([P, ng, P], BF16, tag="fe")
            for g in range(ng):
                nc.tensor.matmul(
                    out=xr[:, g, :],
                    lhsT=spread[:, g0 + g].rearrange("p a b -> p (a b)"),
                    rhs=x_turned[:, h, :],
                    start=True,
                    stop=True,
                )
            engine(
                out=x_rep[:, h, g0 : g0 + ng].rearrange("p g m -> p (g m)").bitcast(F32),
                in_=xr[:].rearrange("p g m -> p (g m)").bitcast(F32),
            )

        def pair_up(pairs, by_plane, g0, ng):
            for u in range(2):
                nc.scalar.copy(
                    out=by_pass_and_byte(pairs)[:, g0 : g0 + ng, u],
                    in_=by_plane[:, 2 * u : 2 * u + 2, g0 * DL : (g0 + ng) * DL].rearrange("p e (g b) -> p g b e", b=DL),
                )

        def step_plane(ab, U, a, first, count_of):
            g0 = blocks[U][1] + first
            return lambda: nc.vector.tensor_scalar(
                out=ab[:, a, first : first + count_of],
                in0=x_rep[:, blocks[U][0], g0 : g0 + count_of, :],
                scalar1=wn[:, 4 + a : 5 + a],
                scalar2=None,
                op0=ALU.is_ge,
            )

        def steps(U, parts=1):
            ab = three_bufs.tile([P, PACK, blocks[U][2], P], BF16, tag="above_then_rows")
            above[U] = ab
            width = blocks[U][2] // parts
            return [step_plane(ab, U, a, part * width, width) for part in range(parts) for a in range(PACK)]

        def sums(j):
            U = j // 2
            gp = psum_fe.tile([P, 4, P], F32, tag="fe")
            summed[j] = gp
            for gi in range(4):
                g = 4 * (j % 2) + gi
                for b in range(PACK):
                    nc.tensor.matmul(
                        out=gp[:, gi, :],
                        lhsT=above[U][:, b, g, :],
                        rhs=table[:, b].rearrange("p a f -> p (a f)"),
                        start=(b == 0),
                        stop=False,
                    )
                nc.tensor.matmul(
                    out=gp[:, gi, :],
                    lhsT=x_rep[:, blocks[U][0], blocks[U][1] + g, :],
                    rhs=x_table[:].rearrange("p a f -> p (a f)"),
                    start=False,
                    stop=True,
                )

        def take(j):
            U, a = unit_of(j)
            du = units[U][2] * DL
            if a == 0:
                gt = keep.tile([P, 12, du], F32, name="got%d" % U)
                qp = keep.tile([P, 5, du], BF16, name="q_planes%d" % U)
                qt = keep.tile([P, units[U][2] * 2 * DL, 2], BF16, name="q_pairs%d" % U)
                got[U], q_planes[U], q_pairs[U] = gt, qp, qt
            cols = slice(a * DL, (a + 4) * DL)
            by_value = summed[j][:].rearrange("p g (a f) -> p f g a", f=16)
            nc.scalar.copy(out=got[U][:, :, cols].rearrange("p f (g a) -> p f g a", a=DL), in_=by_value[:, 0:12])
            nc.scalar.copy(out=q_planes[U][:, 0:4, cols].rearrange("p f (g a) -> p f g a", a=DL), in_=by_value[:, 12:16])
            nc.scalar.activation(
                out=q_planes[U][:, 4, cols].rearrange("p (g a) -> p g a", a=DL), in_=by_value[:, 12], func=ACT.Copy, bias=-1.0
            )
            pair_up(q_pairs[U], q_planes[U], a, 4)

        def spans(U):
            du = units[U][2] * DL
            gt, qp = got[U], q_planes[U]

            def planes(ap, n):
                return ap.unsqueeze(1).to_broadcast([P, n, du])

            ds = two_bufs.tile([P, 6, du], F32, tag="ds")
            turn = two_bufs.tile([P, 2, 4, du], BF16, tag="turn")
            inv = two_bufs.tile([P, 4, du], F32, tag="inv")
            mono = two_bufs.tile([P, 4, du], F32, tag="mono")
            root = temp.tile([P, 4, du], F32, tag="root")
            span3 = temp.tile([P, 3, du], F32, tag="span3")
            span2 = temp.tile([P, 2, du], F32, tag="span2")
            span1 = temp.tile([P, du], F32, tag="span1")
            pair = temp.tile([P, 2, du], F32, tag="pair")
            denom = temp.tile([P, 4, du], F32, tag="denom")
            dist[U], turns[U], invs[U], monos[U] = ds, turn, inv, mono
            return [
                tt(ds[:], gt[:, 0:6, :], gt[:, 6:12, :], ALU.add),
                tt(
                    turn[:],
                    qp[:, 0:4, :].unsqueeze(1).to_broadcast([P, 2, 4, du]),
                    qp[:, 1:5, :].unsqueeze(1).to_broadcast([P, 2, 4, du]),
                    ALU.subtract,
                ),
                both(
                    tt(span2[:], ds[:, 3:5, :], ds[:, 1:3, :], ALU.add),
                    lambda: nc.scalar.activation(out=mono[:, 0, :], in_=ds[:, 3, :], func=ACT.Square),
                    lambda: nc.scalar.activation(out=mono[:, 2, :], in_=ds[:, 2, :], func=ACT.Square),
                ),
                tt(span1[:], ds[:, 3, :], ds[:, 2, :], ALU.add),
                tt(span3[:], ds[:, 3:6, :], ds[:, 0:3, :], ALU.add),
                tt(pair[:], span2[:], planes(span1[:], 2), ALU.mult),
                tt(mono[:, 1:4:2, :], ds[:, 1:3, :], ds[:, 3:5, :], ALU.mult),
                tt(denom[:, 0:2, :], span3[:, 0:2, :], planes(pair[:, 0, :], 2), ALU.mult),
                both(
                    tt(denom[:, 2:4, :], span3[:, 2:0:-1, :], planes(pair[:, 1, :], 2), ALU.mult),
                    lambda: nc.scalar.activation(out=root[:], in_=denom[:], func=ACT.Abs_reciprocal_sqrt),
                    lambda: nc.scalar.activation(out=inv[:], in_=root[:], func=ACT.Square),
                ),
            ]

        def values(U):
            ng = units[U][2]
            du = ng * DL
            ds, turn, inv, mono = dist[U], turns[U], invs[U], monos[U]
            vals = temp.tile([P, 4, du], BF16, tag="vals")
            parts = temp.tile([P, 4, 4, du], BF16, tag="spread_then_parts")
            halfway = temp.tile([P, 2, 4, du], BF16, tag="halfway")
            by_byte = temp.tile([P, 4, du], BF16, tag="by_byte")
            vt = two_bufs.tile([P, ng * 2 * DL, 2], BF16, tag="v_pairs")
            v_pairs[U] = vt
            tm = terms[:, :, 0:du]
            chain = [
                tt(mono[:], mono[:], inv[:], ALU.mult),
                tt(mono[:, 1, :], mono[:, 1, :], mono[:, 3, :], ALU.add),
                tt(
                    tm[:, 1:7, :].rearrange("p (s k) d -> p s k d", k=3),
                    mono[:, 0:3, :].unsqueeze(1).to_broadcast([P, 2, 3, du]),
                    ds[:].rearrange("p (s k) d -> p s k d", k=3),
                    ALU.mult,
                ),
                tt(vals[:], tm[:, 0:4, :], tm[:, 4:8, :], ALU.add),
            ]
            for v in range(4):
                chain.append(
                    tt(
                        parts[:, v],
                        vals[:, v, :].unsqueeze(1).to_broadcast([P, 4, du]),
                        turn[:].rearrange("p r a d -> p (r a) d")[:, 3 - v : 7 - v, :],
                        ALU.mult,
                    )
                )
            chain.append(tt(halfway[:], parts[:, 0:4:2], parts[:, 1:4:2], ALU.add))
            chain.append(
                both(
                    tt(by_byte[:], halfway[:, 0], halfway[:, 1], ALU.add),
                    lambda: pair_up(vt, by_byte, 0, ng),
                )
            )
            return chain

        def knot_table():
            rep_ps = psum_fe.tile([P, 3, 4], F32, tag="fe")
            for a in range(3):
                nc.tensor.matmul(
                    out=rep_ps[:, a, :],
                    lhsT=sel[:, a].rearrange("p a b -> p (a b)"),
                    rhs=knot_rows[:],
                    start=True,
                    stop=True,
                )
            step = keep.tile([P, 9], F32)
            halves = keep.tile([P, 2, 9], BF16)
            chain = [
                cast(
                    wn[:].rearrange("p (a c) -> p a c", c=4),
                    rep_ps[:],
                ),
                lambda: nc.vector.scalar_tensor_tensor(
                    out=step[:], in0=wn[:, 1:10], scalar=minus_later[:], in1=wn[:, 2:11], op0=ALU.mult, op1=ALU.add
                ),
                cast(halves[:, 0, :], step[:]),
                tt(halves[:, 1, :], step[:], halves[:, 0, :], ALU.subtract),
            ]
            for a in range(PACK):
                chain.append(
                    tt(
                        row[:, a, 0:12].rearrange("p (b f) -> p b f", f=6),
                        halves[:, :, a : a + 6],
                        sign[:, a, :].unsqueeze(1).to_broadcast([P, 2, 6]),
                        ALU.mult,
                    )
                )
            chain.append(
                tt(
                    table[:],
                    row[:].unsqueeze(2).to_broadcast([P, PACK, DL, 16]),
                    own_d[:].unsqueeze(1).unsqueeze(3).to_broadcast([P, PACK, DL, 16]),
                    ALU.mult,
                )
            )
            return chain

        rows = CHUNK * 2 * DL

        def first_pass(c):
            return (c % chunks_per_half) * CHUNK

        def part_of(c):
            U, g = unit_of(c)
            return U, slice(g * 2 * DL, g * 2 * DL + rows)

        def mask(c):
            U, part = part_of(c)
            yr = three_bufs.tile([P, rows, JQ, 2], BF16, tag="above_then_rows")
            y_rows[c] = yr
            nc.vector.tensor_tensor(
                out=yr[:],
                in0=q_pairs[U][:, part, :].unsqueeze(2).to_broadcast([P, rows, JQ, 2]),
                in1=count[:].unsqueeze(1).to_broadcast([P, rows, JQ, 2]),
                op=ALU.is_equal,
            )

        def fill(c):
            U, part = part_of(c)
            yr, g0 = y_rows[c], first_pass(c)
            nc.vector.tensor_tensor(
                out=yr[:],
                in0=yr[:],
                in1=v_pairs[U][:, part, :].unsqueeze(2).to_broadcast([P, rows, JQ, 2]),
                op=ALU.mult,
            )
            nc.scalar.copy(
                out=yr[:].rearrange("p (g u b) j e -> p g u b j e", u=2, b=DL)[:, :, 1, :, JQ - 1, 1],
                in_=silu_sb[c // chunks_per_half][:, g0 * DL : (g0 + CHUNK) * DL].rearrange("p (g b) -> p g b", b=DL),
            )

        def flip(c):
            y_words = y_rows[c][:].rearrange("p c j e -> p (c j e)").bitcast(F32)
            gr = two_bufs.tile([P, CHUNK, P, PACK], BF16, tag="grouped", align_bytes=64)
            for b in range(CHUNK // 2):
                yt = psum_fe.tile([P, 2, 2, P], F32, tag="fe")
                for u in range(2):
                    for gi in range(2):
                        col = ((2 * b + gi) * 2 + u) * P
                        nc.tensor.transpose(out=yt[:, gi, u, :], in_=y_words[:, col : col + P], identity=ident_words[:])
                nc.scalar.copy(out=gr[:, 2 * b : 2 * b + 2].bitcast(F32), in_=yt[:].rearrange("p g u m -> p g m u"))
            grouped[c] = gr

        def quantise(c, first=0, count_of=CHUNK):
            g0 = first_pass(c) + first
            nc.vector.quantize_mx(
                out=y_codes[:, g0 : g0 + count_of, :].rearrange("p g m -> p (g m)").bitcast(FP8X4),
                scales=y_planes[:, g0 : g0 + count_of, :].rearrange("p g m -> p (g m)"),
                in_=grouped[c][:, first : first + count_of].rearrange("p g m a -> p (g m a)"),
            )

        def multiply(c, first=0, count_of=CHUNK):
            h, g0 = c // chunks_per_half, first_pass(c) + first
            if g0 == 0:
                for nu in range(N_TILES):
                    acc_nu = psum_acc.tile([P, N_TILE], F32, name="acc%d" % nu)
                    acc[(h, nu)] = acc_nu
            passes = range(g0, g0 + count_of)
            if h == 0:
                order = [(g, nu) for g in passes for nu in range(N_TILES)]
            else:
                order = [(g, nu) for nu in range(N_TILES) for g in passes]
            for g, nu in order:
                cols = slice(nu * N_TILE, (nu + 1) * N_TILE)
                nc.tensor.matmul_mx(
                    out=acc[(h, nu)][:],
                    lhsT=y_codes[:, g, :].bitcast(FP8X4),
                    lhsT_scale=y_planes[:, g, :],
                    rhs=w_codes[g][:, cols].bitcast(FP8X4),
                    rhs_scale=w_planes[4 * (g % 4) : P, g // 4, cols],
                    start=(g == 0),
                    stop=(g == PASSES - 1),
                )

        def store(h):
            result = temp.tile([P, N_TILES, N_TILE], F32, tag="x_rep_then_results")
            for nu in range(N_TILES):
                nc.scalar.copy(out=result[:, nu, :], in_=acc[(h, nu)][:])
                nc.sync.dma_start(out=out[h * P : (h + 1) * P, nu * N_TILE : (nu + 1) * N_TILE], in_=result[:, nu, :])

        def take_turns(one, other):
            merged = []
            for i in range(max(len(one), len(other))):
                merged.extend(one[i : i + 1])
                merged.extend(other[i : i + 1])
            return merged

        warm = keep.tile([P, 2], F32)
        nc.scalar.activation(out=warm[:, 0:1], in_=first[:], func=ACT.Silu)
        silu_sb = []
        for h in range(HALVES):
            silu_half = keep.tile([P, D], BF16, name="silu_half%d" % h)
            nc.scalar.activation(out=silu_half[:], in_=x_sb[h], func=ACT.Silu)
            silu_sb.append(silu_half)
        nc.scalar.activation(out=warm[:, 1:2], in_=first[:], func=ACT.Abs_reciprocal_sqrt, bias=1.0)
        first_of = dict((4 * units[U][0] + units[U][1] // CHUNK, U) for U in range(n_units))
        last_of = dict((4 * units[U][0] + (units[U][1] + units[U][2]) // CHUNK - 1, U) for U in range(n_units))
        masked = set()

        def need_mask(c):
            if c < n_chunks and c not in masked:
                mask(c)
                masked.add(c)

        left = {}

        def lace(chain, other):
            laced, at = [], 0
            for i in range(len(chain)):
                laced.append(chain[i])
                if i in (0, 1, 2, 3, 7, 8) and at < len(other):
                    laced.append(other[at])
                    at += 1
            return laced, other[at:]

        def prepare(c):
            need_mask(c)
            if c in first_of:
                U = first_of[c]
                if U >= 1 and U + 1 < n_units:
                    laced, left[U + 1] = lace(values(U), spans(U + 1))
                    run(laced)
                else:
                    run(values(U))
                need_mask(c + 1)
            fill(c)
            if c in last_of and last_of[c] + 1 < n_units:
                run(left[last_of[c] + 1] if last_of[c] + 1 in left else spans(last_of[c] + 1))

        turn_x()
        table_chain = knot_table()
        run(table_chain[:4])
        replicate(0, nc.vector.tensor_copy)
        run(table_chain[4:])
        for U in range(1, len(blocks)):
            replicate(U, nc.scalar.copy)
        run(steps(0, 2))
        sums(0)
        sums(1)
        run(steps(1))
        sums(2)
        sums(3)
        take(0)
        take(1)
        run(steps(2))
        sums(4)
        sums(5)
        run(steps(3))
        take(2)
        run(spans(0))
        take(3)
        sums(6)
        sums(7)
        need_mask(0)
        take(4)
        take(5)
        laced, left[1] = lace(values(0), spans(1))
        run(laced)
        need_mask(1)
        take(6)
        fill(0)
        take(7)
        fill(1)
        flip(0)
        run(left[1])
        flip(1)
        need_mask(2)
        quantise(0)
        for c in range(2, n_chunks + 2):
            if c < n_chunks:
                prepare(c)
            multiply(c - 2)
            if (c - 1) % chunks_per_half == 0:
                store((c - 2) // chunks_per_half)
            if c < n_chunks:
                flip(c)
            if c - 1 < n_chunks:
                quantise(c - 1)
